import numpy as np
import ml_dtypes

BF16 = ml_dtypes.bfloat16


def bf(x):
    return np.asarray(x, np.float32).astype(BF16)


def f32(x):
    return np.asarray(x, np.float32)


def f64(x):
    return np.asarray(x).astype(np.float64)


def striped(idx):
    return np.tile(idx.reshape(-1, 16).T, (8, 1))


S, D, H, O, M, N = 4096, 128, 4, 128, 512, 2048
SLOPE, DENS, HS = 0.2, 0.03125, 2.0


def setup_inputs():
    table = bf(np.random.standard_normal((S, D)))
    w = bf(HS * np.random.standard_normal((D, M)) / np.sqrt(D))
    a_src = bf(np.random.standard_normal((M, 1)) / (HS * np.sqrt(O)))
    a_dst = bf(np.random.standard_normal((M, 1)) / (HS * np.sqrt(O)))
    adj = (np.random.random((N, N)) < DENS).astype(np.float32)
    np.fill_diagonal(adj, 1.0)
    return {"table": table, "w": w, "a_src": a_src, "a_dst": a_dst, "adj_t": bf(adj), "offs": striped(np.random.permutation(S)[:N])}


def reference(table, w, a_src, a_dst, adj_t, offs):
    idx = offs[:16].T.reshape(-1)
    hf = f64(w).T @ f64(table)[idx].T
    mask = f64(adj_t)
    y = np.zeros((M, N))
    for q in range(H):
        r = slice(q * O, (q + 1) * O)
        hq = hf[r]
        s_src = f64(a_src)[r, 0] @ hq
        s_dst = f64(a_dst)[r, 0] @ hq
        u = s_dst[:, None] + s_src[None, :]
        p = mask * np.exp(np.maximum(u, SLOPE * u))
        y[r] = (hq @ p) / p.sum(axis=0)[None, :]
    return np.maximum(y, 0.0) + np.exp(np.minimum(y, 0.0)) - 1.0

@@ -1,0 +1,191 @@
+import concourse.mybir as mybir
+from concourse.masks import make_identity
+
+BF16 = mybir.dt.bfloat16
+F32 = mybir.dt.float32
+U16 = mybir.dt.uint16
+FUNC = mybir.ActivationFunctionType
+ALU = mybir.AluOpType
+
+P = 128
+S, D, H, O, N = 4096, 128, 4, 128, 2048
+SLOPE = 0.2
+PIECE = 512
+BLOCKS = N // P
+UNIT = 1024
+ROW = 136
+SUMS = 130
+
+FLOPS = 2 * D * H * O * N + 2 * 2 * H * O * N + 2 * H * N * N * (O + 1)
+
+
+def tile_multiheadgraphchannelattention_b_kernel(tc, table, w, a_src, a_dst, adj_t, offs, out):
+    nc = tc.nc
+    with (
+        tc.tile_pool(name="lists", bufs=1) as lists,
+        tc.tile_pool(name="held", bufs=1) as held,
+        tc.tile_pool(name="ring", bufs=2) as ring,
+        tc.tile_pool(name="weights_of_sum", bufs=2 * BLOCKS) as weights_of_sum,
+    ):
+        offsets = lists.tile([P, N // 16], U16, name="offsets")
+        nc.sync.dma_start(offsets[:], offs)
+
+        table_blocks = table.rearrange("(b p) d -> p b d", p=P)
+        raw_chunks = []
+        for c in range(4):
+            raw = ring.tile([P, 8, D], BF16, name="raw", bufs=4)
+            nc.sync.dma_start(raw[:], table_blocks[:, 8 * c : 8 * c + 8, :])
+            raw_chunks.append(raw)
+
+        proj = held.tile([D, H * O], BF16, name="proj")
+        nc.scalar.dma_start(proj[:], w)
+        a_rows = held.tile([P, O], BF16, name="a_rows")
+        nc.scalar.dma_start(a_rows[0:H, :], a_src.rearrange("(q o) one -> q (o one)", q=H))
+        nc.scalar.dma_start(a_rows[H : 2 * H, :], a_dst.rearrange("(q o) one -> q (o one)", q=H))
+
+        adj = []
+        for tb in range(BLOCKS):
+            adj_rows = held.tile([P, N], BF16, name=f"adj{tb}")
+            queue = nc.sync if tb % 2 == 0 else nc.scalar
+            queue.dma_start(adj_rows[:], adj_t[tb * P : (tb + 1) * P, :])
+            adj.append(adj_rows)
+
+        ident_bf = held.tile([P, P], BF16, name="ident_bf")
+        make_identity(nc, ident_bf[:])
+        ident_f = held.tile([P, P], F32, name="ident_f")
+        make_identity(nc, ident_f[:])
+
+        hf_t = []
+        for q in range(H):
+            blocks_t = held.tile([P, BLOCKS * ROW], BF16, name=f"hf_t{q}")
+            nc.gpsimd.memset(blocks_t[:], 1.0)
+            hf_t.append(blocks_t)
+
+        table_t = held.tile([D, S], BF16, name="table_t")
+        hf = [held.tile([O, N], BF16, name=f"hf{q}") for q in range(H)]
+        c_row = [held.tile([P, N], F32, name=f"c_row{q}") for q in range(H)]
+        b_col = [held.tile([P, BLOCKS], F32, name=f"b_col{q}") for q in range(H)]
+        e_col = [held.tile([P, BLOCKS], F32, name=f"e_col{q}") for q in range(H)]
+
+        with tc.psum_pool(name="psum_first", bufs=2) as psum_first:
+            a_cols_ps = psum_first.tile([P, 8 * P], BF16, name="a_cols_ps", tag="flipped")
+            nc.tensor.transpose(a_cols_ps[:, 0 : 2 * H], a_rows[0 : 2 * H, :], ident_bf[0 : 2 * H, 0 : 2 * H])
+            a_cols = held.tile([O, 2 * H], BF16, name="a_cols")
+            nc.vector.tensor_copy(a_cols[:], a_cols_ps[:, 0 : 2 * H])
+            a_src_wide = held.tile([O, H * P], BF16, name="a_src_wide")
+            for q in range(H):
+                nc.vector.tensor_copy(a_src_wide[:, q * P : (q + 1) * P], a_cols[:, q : q + 1].to_broadcast([O, P]))
+
+            for c in range(4):
+                flipped = psum_first.tile([P, 8 * P], BF16, name="flipped")
+                for k in range(8):
+                    nc.tensor.transpose(flipped[:, k * P : (k + 1) * P], raw_chunks[c][:, k, :], ident_bf[:])
+                if c % 2 == 0:
+                    nc.vector.tensor_copy(table_t[:, c * 8 * P : (c + 1) * 8 * P], flipped[:])
+                else:
+                    nc.scalar.copy(table_t[:, c * 8 * P : (c + 1) * 8 * P], flipped[:])
+
+            for q in range(H):
+                for c in range(N // PIECE):
+                    picked = table_t[:].indirect(offsets[:, c * (PIECE // 16) : (c + 1) * (PIECE // 16)])
+                    product = psum_first.tile([O, PIECE], F32, name="product", bufs=6)
+                    nc.tensor.matmul(product[:], proj[:, q * O : (q + 1) * O], picked, start=True, stop=True)
+                    if c % 2 == 0:
+                        nc.vector.tensor_copy(hf[q][:, c * PIECE : (c + 1) * PIECE], product[:])
+                    else:
+                        nc.scalar.copy(hf[q][:, c * PIECE : (c + 1) * PIECE], product[:])
+
+            for q in range(H):
+                for c in range(N // PIECE):
+                    s_src = psum_first.tile([P, PIECE], F32, name="s_src", tag="product", bufs=6)
+                    nc.tensor.matmul(
+                        s_src[:], a_src_wide[:, q * P : (q + 1) * P], hf[q][:, c * PIECE : (c + 1) * PIECE],
+                        start=True, stop=True,
+                    )
+                    nc.scalar.activation(c_row[q][:, c * PIECE : (c + 1) * PIECE], s_src[:], FUNC.Exp, scale=SLOPE - 1.0)
+                s_dst = psum_first.tile([P, BLOCKS], F32, name="s_dst", tag="product", bufs=6)
+                for tb in range(BLOCKS):
+                    nc.tensor.matmul(
+                        s_dst[:, tb : tb + 1], hf[q][:, tb * P : (tb + 1) * P], a_cols[:, H + q : H + q + 1],
+                        start=True, stop=True,
+                    )
+                nc.scalar.activation(b_col[q][:], s_dst[:], FUNC.Exp)
+                nc.scalar.activation(e_col[q][:], s_dst[:], FUNC.Exp, scale=SLOPE)
+                rows_t = hf_t[q].rearrange("p (b c) -> p b c", c=ROW)
+                for half in range(2):
+                    flipped = psum_first.tile([P, 8 * P], BF16, name="flipped")
+                    for k in range(8):
+                        tb = 8 * half + k
+                        nc.tensor.transpose(flipped[:, k * P : (k + 1) * P], hf[q][:, tb * P : (tb + 1) * P], ident_bf[:])
+                    nc.scalar.copy(rows_t[:, 8 * half : 8 * half + 8, 0:O], flipped.rearrange("p (b c) -> p b c", c=P))
+
+        with tc.psum_pool(name="psum_sums", bufs=2) as psum_sums:
+
+            def make_weights(unit):
+                q, cols = unit // 2, slice((unit % 2) * UNIT, (unit % 2 + 1) * UNIT)
+                tiles = []
+                for tb in range(BLOCKS):
+                    unmasked = ring.tile([P, UNIT], BF16, name="unmasked")
+                    nc.vector.tensor_scalar(
+                        unmasked[:], c_row[q][:, cols], e_col[q][:, tb : tb + 1], b_col[q][:, tb : tb + 1],
+                        ALU.mult, ALU.max,
+                    )
+                    weights = weights_of_sum.tile([P, UNIT], BF16, name="weights")
+                    nc.vector.tensor_tensor(weights[:], unmasked[:], adj[tb][:, cols], ALU.mult)
+                    tiles.append(weights)
+                return tiles
+
+            def sum_pair(unit, tiles, pair):
+                q = unit // 2
+                sums = psum_sums.tile([P, 2 * SUMS], F32, name="sums", bufs=4)
+                for k in range(2):
+                    jb = 2 * pair + k
+                    for tb in range(BLOCKS):
+                        nc.tensor.matmul(
+                            sums[:, k * SUMS : k * SUMS + O + 1],
+                            tiles[tb][:, jb * P : (jb + 1) * P],
+                            hf_t[q][:, tb * ROW : tb * ROW + O + 1],
+                            start=(tb == 0), stop=(tb == BLOCKS - 1),
+                        )
+                return sums
+
+            def divide_and_flip(sums, y_t, pair):
+                recip = ring.tile([P, 2], F32, name="recip", bufs=4)
+                nc.vector.reciprocal(recip[:].unsqueeze(2), sums.rearrange("p (k c) -> p k c", c=SUMS)[:, :, O : O + 1])
+                y = ring.tile([P, 2 * O], F32, name="y", bufs=3)
+                for k in range(2):
+                    nc.scalar.activation(
+                        y[:, k * O : (k + 1) * O], sums[:, k * SUMS : k * SUMS + O], FUNC.Copy, scale=recip[:, k : k + 1]
+                    )
+                for k in range(2):
+                    at = (2 * (pair % 2) + k) * P
+                    nc.tensor.transpose(y_t[:, at : at + P], y[:, k * O : (k + 1) * O], ident_f[:])
+
+            def elu_and_store(unit, y_t, half):
+                q, first = unit // 2, (unit % 2) * UNIT + half * 4 * P
+                e = ring.tile([O, 4 * P], F32, name="e")
+                nc.scalar.activation(e[:], y_t[:], FUNC.Relu, scale=-1.0)
+                nc.scalar.activation(e[:], e[:], FUNC.Exp, scale=-1.0)
+                result = ring.tile([O, 4 * P], F32, name="result")
+                nc.vector.scalar_tensor_tensor(result[:], e[:], -1.0, y_t[:], ALU.add, ALU.max)
+                nc.sync.dma_start(out[q * O : (q + 1) * O, first : first + 4 * P], result[:])
+
+            def sum_unit(unit, tiles):
+                waiting = None
+                y_t = None
+                for pair in range(UNIT // (2 * P) + 1):
+                    sums = sum_pair(unit, tiles, pair) if pair < UNIT // (2 * P) else None
+                    if waiting is not None:
+                        if (pair - 1) % 2 == 0:
+                            y_t = psum_sums.tile([O, 4 * P], F32, name="y_t")
+                        divide_and_flip(waiting, y_t, pair - 1)
+                        if (pair - 1) % 2 == 1:
+                            elu_and_store(unit, y_t, (pair - 1) // 2)
+                    waiting = sums
+
+            units = H * N // UNIT
+            made = make_weights(0)
+            for unit in range(units):
+                ahead = make_weights(unit + 1) if unit + 1 < units else None
+                sum_unit(unit, made)
+                made = ahead

@@ -13,6 +13,8 @@ SLOPE = 0.2
 PIECE = 512
 BLOCKS = N // P
 UNIT = 1024
+BY_SCALAR = 320
+BY_VECTOR = UNIT - BY_SCALAR
 ROW = 136
 SUMS = 130
 
@@ -63,9 +65,12 @@ def tile_multiheadgraphchannelattention_b_kernel(tc, table, w, a_src, a_dst, adj
 
         table_t = held.tile([D, S], BF16, name="table_t")
         hf = [held.tile([O, N], BF16, name=f"hf{q}") for q in range(H)]
-        c_row = [held.tile([P, N], F32, name=f"c_row{q}") for q in range(H)]
+        c_row = [held.tile([P, (N // UNIT) * BY_VECTOR], F32, name=f"c_row{q}") for q in range(H)]
+        s_row = [held.tile([P, (N // UNIT) * BY_SCALAR], F32, name=f"s_row{q}") for q in range(H)]
         b_col = [held.tile([P, BLOCKS], F32, name=f"b_col{q}") for q in range(H)]
         e_col = [held.tile([P, BLOCKS], F32, name=f"e_col{q}") for q in range(H)]
+        d_col = [held.tile([P, BLOCKS], F32, name=f"d_col{q}") for q in range(H)]
+        n_col = [held.tile([P, BLOCKS], F32, name=f"n_col{q}") for q in range(H)]
 
         with tc.psum_pool(name="psum_first", bufs=2) as psum_first:
             a_cols_ps = psum_first.tile([P, 8 * P], BF16, name="a_cols_ps", tag="flipped")
@@ -102,7 +107,12 @@ def tile_multiheadgraphchannelattention_b_kernel(tc, table, w, a_src, a_dst, adj
                         s_src[:], a_src_wide[:, q * P : (q + 1) * P], hf[q][:, c * PIECE : (c + 1) * PIECE],
                         start=True, stop=True,
                     )
-                    nc.scalar.activation(c_row[q][:, c * PIECE : (c + 1) * PIECE], s_src[:], FUNC.Exp, scale=SLOPE - 1.0)
+                    unit_of_head, second = c // 2, c % 2
+                    kept = 0 if second else BY_SCALAR
+                    if kept:
+                        nc.scalar.copy(s_row[q][:, unit_of_head * BY_SCALAR : (unit_of_head + 1) * BY_SCALAR], s_src[:, 0:kept])
+                    at = unit_of_head * BY_VECTOR + (PIECE - BY_SCALAR if second else 0)
+                    nc.scalar.activation(c_row[q][:, at : at + PIECE - kept], s_src[:, kept:PIECE], FUNC.Exp, scale=SLOPE - 1.0)
                 s_dst = psum_first.tile([P, BLOCKS], F32, name="s_dst", tag="product", bufs=6)
                 for tb in range(BLOCKS):
                     nc.tensor.matmul(
@@ -111,6 +121,8 @@ def tile_multiheadgraphchannelattention_b_kernel(tc, table, w, a_src, a_dst, adj
                     )
                 nc.scalar.activation(b_col[q][:], s_dst[:], FUNC.Exp)
                 nc.scalar.activation(e_col[q][:], s_dst[:], FUNC.Exp, scale=SLOPE)
+                nc.scalar.copy(d_col[q][:], s_dst[:])
+                nc.scalar.mul(n_col[q][:], s_dst[:], SLOPE - 1.0)
                 rows_t = hf_t[q].rearrange("p (b c) -> p b c", c=ROW)
                 for half in range(2):
                     flipped = psum_first.tile([P, 8 * P], BF16, name="flipped")
@@ -122,13 +134,20 @@ def tile_multiheadgraphchannelattention_b_kernel(tc, table, w, a_src, a_dst, adj
         with tc.psum_pool(name="psum_sums", bufs=2) as psum_sums:
 
             def make_weights(unit):
-                q, cols = unit // 2, slice((unit % 2) * UNIT, (unit % 2 + 1) * UNIT)
+                q, half = unit // 2, unit % 2
+                cols = slice(half * UNIT, (half + 1) * UNIT)
                 tiles = []
                 for tb in range(BLOCKS):
-                    unmasked = ring.tile([P, UNIT], BF16, name="unmasked")
+                    unmasked = ring.tile([P, UNIT], BF16, name="unmasked", bufs=4)
+                    ramp = ring.tile([P, BY_SCALAR], F32, name="ramp", bufs=3)
+                    nc.scalar.activation(
+                        ramp[:], s_row[q][:, half * BY_SCALAR : (half + 1) * BY_SCALAR], FUNC.Relu,
+                        bias=n_col[q][:, tb : tb + 1], scale=SLOPE - 1.0,
+                    )
+                    nc.scalar.activation(unmasked[:, 0:BY_SCALAR], ramp[:], FUNC.Exp, bias=d_col[q][:, tb : tb + 1])
                     nc.vector.tensor_scalar(
-                        unmasked[:], c_row[q][:, cols], e_col[q][:, tb : tb + 1], b_col[q][:, tb : tb + 1],
-                        ALU.mult, ALU.max,
+                        unmasked[:, BY_SCALAR:UNIT], c_row[q][:, half * BY_VECTOR : (half + 1) * BY_VECTOR],
+                        e_col[q][:, tb : tb + 1], b_col[q][:, tb : tb + 1], ALU.mult, ALU.max,
                     )
                     weights = weights_of_sum.tile([P, UNIT], BF16, name="weights")
                     nc.vector.tensor_tensor(weights[:], unmasked[:], adj[tb][:, cols], ALU.mult)

@@ -11,14 +11,21 @@ P = 128
 S, D, H, O, N = 4096, 128, 4, 128, 2048
 SLOPE = 0.2
 PIECE = 512
+PIECES = N // PIECE
 BLOCKS = N // P
-UNIT = 1024
-BY_SCALAR = 320
-BY_VECTOR = UNIT - BY_SCALAR
+NODES_A_ROW = 8
+CHUNKS = S // (P * NODES_A_ROW)
+BY_SCALAR = 144
+BY_VECTOR = PIECE - BY_SCALAR
 ROW = 136
 SUMS = 130
+UNITS = [(q, c, 2) for q in range(H) for c in (0, 2)][:-1] + [(H - 1, 2, 1), (H - 1, 3, 1)]
 
 FLOPS = 2 * D * H * O * N + 2 * 2 * H * O * N + 2 * H * N * N * (O + 1)
+
+
+def runs_of(ap, width):
+    return ap.rearrange("p (r k) -> p r k", k=width)
 
 
 def tile_multiheadgraphchannelattention_b_kernel(tc, table, w, a_src, a_dst, adj_t, offs, out):
@@ -32,11 +39,11 @@ def tile_multiheadgraphchannelattention_b_kernel(tc, table, w, a_src, a_dst, adj
         offsets = lists.tile([P, N // 16], U16, name="offsets")
         nc.sync.dma_start(offsets[:], offs)
 
-        table_blocks = table.rearrange("(b p) d -> p b d", p=P)
+        table_chunks = table.rearrange("(c p r) d -> c p r d", p=P, r=NODES_A_ROW)
         raw_chunks = []
-        for c in range(4):
-            raw = ring.tile([P, 8, D], BF16, name="raw", bufs=4)
-            nc.sync.dma_start(raw[:], table_blocks[:, 8 * c : 8 * c + 8, :])
+        for c in range(CHUNKS):
+            raw = ring.tile([P, NODES_A_ROW, D], BF16, name="raw", bufs=CHUNKS)
+            nc.sync.dma_start(raw[:], table_chunks[c])
             raw_chunks.append(raw)
 
         proj = held.tile([D, H * O], BF16, name="proj")
@@ -44,12 +51,14 @@ def tile_multiheadgraphchannelattention_b_kernel(tc, table, w, a_src, a_dst, adj
         a_rows = held.tile([P, O], BF16, name="a_rows")
         nc.scalar.dma_start(a_rows[0:H, :], a_src.rearrange("(q o) one -> q (o one)", q=H))
         nc.scalar.dma_start(a_rows[H : 2 * H, :], a_dst.rearrange("(q o) one -> q (o one)", q=H))
+        warm = held.tile([P, 1], F32, name="warm")
+        nc.vector.memset(warm[:], 0.0)
+        nc.scalar.activation(warm[:], warm[:], FUNC.Exp)
 
         adj = []
         for tb in range(BLOCKS):
             adj_rows = held.tile([P, N], BF16, name=f"adj{tb}")
-            queue = nc.sync if tb % 2 == 0 else nc.scalar
-            queue.dma_start(adj_rows[:], adj_t[tb * P : (tb + 1) * P, :])
+            nc.sync.dma_start(adj_rows[:], adj_t[tb * P : (tb + 1) * P, :])
             adj.append(adj_rows)
 
         ident_bf = held.tile([P, P], BF16, name="ident_bf")
@@ -65,15 +74,15 @@ def tile_multiheadgraphchannelattention_b_kernel(tc, table, w, a_src, a_dst, adj
 
         table_t = held.tile([D, S], BF16, name="table_t")
         hf = [held.tile([O, N], BF16, name=f"hf{q}") for q in range(H)]
-        c_row = [held.tile([P, (N // UNIT) * BY_VECTOR], F32, name=f"c_row{q}") for q in range(H)]
-        s_row = [held.tile([P, (N // UNIT) * BY_SCALAR], F32, name=f"s_row{q}") for q in range(H)]
+        c_row = [held.tile([P, PIECES * BY_VECTOR], F32, name=f"c_row{q}") for q in range(H)]
+        s_row = [held.tile([P, PIECES * BY_SCALAR], F32, name=f"s_row{q}") for q in range(H)]
         b_col = [held.tile([P, BLOCKS], F32, name=f"b_col{q}") for q in range(H)]
         e_col = [held.tile([P, BLOCKS], F32, name=f"e_col{q}") for q in range(H)]
         d_col = [held.tile([P, BLOCKS], F32, name=f"d_col{q}") for q in range(H)]
         n_col = [held.tile([P, BLOCKS], F32, name=f"n_col{q}") for q in range(H)]
 
         with tc.psum_pool(name="psum_first", bufs=2) as psum_first:
-            a_cols_ps = psum_first.tile([P, 8 * P], BF16, name="a_cols_ps", tag="flipped")
+            a_cols_ps = psum_first.tile([P, NODES_A_ROW * P], BF16, name="a_cols_ps", tag="flipped")
             nc.tensor.transpose(a_cols_ps[:, 0 : 2 * H], a_rows[0 : 2 * H, :], ident_bf[0 : 2 * H, 0 : 2 * H])
             a_cols = held.tile([O, 2 * H], BF16, name="a_cols")
             nc.vector.tensor_copy(a_cols[:], a_cols_ps[:, 0 : 2 * H])
@@ -81,17 +90,19 @@ def tile_multiheadgraphchannelattention_b_kernel(tc, table, w, a_src, a_dst, adj
             for q in range(H):
                 nc.vector.tensor_copy(a_src_wide[:, q * P : (q + 1) * P], a_cols[:, q : q + 1].to_broadcast([O, P]))
 
-            for c in range(4):
-                flipped = psum_first.tile([P, 8 * P], BF16, name="flipped")
-                for k in range(8):
-                    nc.tensor.transpose(flipped[:, k * P : (k + 1) * P], raw_chunks[c][:, k, :], ident_bf[:])
+            for c in range(CHUNKS):
+                flipped = psum_first.tile([P, NODES_A_ROW * P], BF16, name="flipped")
+                for r in range(NODES_A_ROW):
+                    nc.tensor.transpose(flipped[:, r * P : (r + 1) * P], raw_chunks[c][:, r, :], ident_bf[:])
+                in_order = flipped.rearrange("d (r p) -> d p r", p=P)
+                window_part = runs_of(table_t[:, c * NODES_A_ROW * P : (c + 1) * NODES_A_ROW * P], NODES_A_ROW)
                 if c % 2 == 0:
-                    nc.vector.tensor_copy(table_t[:, c * 8 * P : (c + 1) * 8 * P], flipped[:])
+                    nc.vector.tensor_copy(window_part, in_order)
                 else:
-                    nc.scalar.copy(table_t[:, c * 8 * P : (c + 1) * 8 * P], flipped[:])
+                    nc.scalar.copy(window_part, in_order)
 
             for q in range(H):
-                for c in range(N // PIECE):
+                for c in range(PIECES):
                     picked = table_t[:].indirect(offsets[:, c * (PIECE // 16) : (c + 1) * (PIECE // 16)])
                     product = psum_first.tile([O, PIECE], F32, name="product", bufs=6)
                     nc.tensor.matmul(product[:], proj[:, q * O : (q + 1) * O], picked, start=True, stop=True)
@@ -100,20 +111,10 @@ def tile_multiheadgraphchannelattention_b_kernel(tc, table, w, a_src, a_dst, adj
                     else:
                         nc.scalar.copy(hf[q][:, c * PIECE : (c + 1) * PIECE], product[:])
 
-            for q in range(H):
-                for c in range(N // PIECE):
-                    s_src = psum_first.tile([P, PIECE], F32, name="s_src", tag="product", bufs=6)
-                    nc.tensor.matmul(
-                        s_src[:], a_src_wide[:, q * P : (q + 1) * P], hf[q][:, c * PIECE : (c + 1) * PIECE],
-                        start=True, stop=True,
-                    )
-                    unit_of_head, second = c // 2, c % 2
-                    kept = 0 if second else BY_SCALAR
-                    if kept:
-                        nc.scalar.copy(s_row[q][:, unit_of_head * BY_SCALAR : (unit_of_head + 1) * BY_SCALAR], s_src[:, 0:kept])
-                    at = unit_of_head * BY_VECTOR + (PIECE - BY_SCALAR if second else 0)
-                    nc.scalar.activation(c_row[q][:, at : at + PIECE - kept], s_src[:, kept:PIECE], FUNC.Exp, scale=SLOPE - 1.0)
-                s_dst = psum_first.tile([P, BLOCKS], F32, name="s_dst", tag="product", bufs=6)
+        with tc.psum_pool(name="psum_sums", bufs=2) as psum_sums:
+
+            def score_columns(q):
+                s_dst = psum_sums.tile([P, BLOCKS], F32, name="s_dst", tag="score")
                 for tb in range(BLOCKS):
                     nc.tensor.matmul(
                         s_dst[:, tb : tb + 1], hf[q][:, tb * P : (tb + 1) * P], a_cols[:, H + q : H + q + 1],
@@ -123,40 +124,66 @@ def tile_multiheadgraphchannelattention_b_kernel(tc, table, w, a_src, a_dst, adj
                 nc.scalar.activation(e_col[q][:], s_dst[:], FUNC.Exp, scale=SLOPE)
                 nc.scalar.copy(d_col[q][:], s_dst[:])
                 nc.scalar.mul(n_col[q][:], s_dst[:], SLOPE - 1.0)
-                rows_t = hf_t[q].rearrange("p (b c) -> p b c", c=ROW)
+
+            def score_rows(q, c):
+                s_src = psum_sums.tile([P, PIECE], F32, name="s_src", tag="score")
+                nc.tensor.matmul(
+                    s_src[:], a_src_wide[:, q * P : (q + 1) * P], hf[q][:, c * PIECE : (c + 1) * PIECE],
+                    start=True, stop=True,
+                )
+                nc.scalar.copy(s_row[q][:, c * BY_SCALAR : (c + 1) * BY_SCALAR], s_src[:, 0:BY_SCALAR])
+                nc.scalar.activation(
+                    c_row[q][:, c * BY_VECTOR : (c + 1) * BY_VECTOR], s_src[:, BY_SCALAR:PIECE], FUNC.Exp, scale=SLOPE - 1.0
+                )
+
+            def flip_head(q):
                 for half in range(2):
-                    flipped = psum_first.tile([P, 8 * P], BF16, name="flipped")
+                    flipped = psum_sums.tile([P, 8 * P], BF16, name="flipped", bufs=1)
                     for k in range(8):
                         tb = 8 * half + k
                         nc.tensor.transpose(flipped[:, k * P : (k + 1) * P], hf[q][:, tb * P : (tb + 1) * P], ident_bf[:])
-                    nc.scalar.copy(rows_t[:, 8 * half : 8 * half + 8, 0:O], flipped.rearrange("p (b c) -> p b c", c=P))
+                    nc.scalar.copy(runs_of(hf_t[q], ROW)[:, 8 * half : 8 * half + 8, 0:O], runs_of(flipped, P))
 
-        with tc.psum_pool(name="psum_sums", bufs=2) as psum_sums:
-
-            def make_weights(unit):
-                q, half = unit // 2, unit % 2
-                cols = slice(half * UNIT, (half + 1) * UNIT)
+            def make_weights(q, first, pieces):
+                width = pieces * PIECE
                 tiles = []
                 for tb in range(BLOCKS):
-                    unmasked = ring.tile([P, UNIT], BF16, name="unmasked", bufs=4)
-                    ramp = ring.tile([P, BY_SCALAR], F32, name="ramp", bufs=3)
+                    unmasked = ring.tile([P, 2 * PIECE], BF16, name="unmasked", bufs=4)
+                    ramp = ring.tile([P, 2 * BY_SCALAR], F32, name="ramp", bufs=3)
                     nc.scalar.activation(
-                        ramp[:], s_row[q][:, half * BY_SCALAR : (half + 1) * BY_SCALAR], FUNC.Relu,
-                        bias=n_col[q][:, tb : tb + 1], scale=SLOPE - 1.0,
+                        ramp[:, 0 : pieces * BY_SCALAR], s_row[q][:, first * BY_SCALAR : (first + pieces) * BY_SCALAR],
+                        FUNC.Relu, bias=n_col[q][:, tb : tb + 1], scale=SLOPE - 1.0,
                     )
-                    nc.scalar.activation(unmasked[:, 0:BY_SCALAR], ramp[:], FUNC.Exp, bias=d_col[q][:, tb : tb + 1])
+                    nc.scalar.activation(
+                        runs_of(unmasked[:, 0:width], PIECE)[:, :, 0:BY_SCALAR],
+                        runs_of(ramp[:, 0 : pieces * BY_SCALAR], BY_SCALAR),
+                        FUNC.Exp, bias=d_col[q][:, tb : tb + 1],
+                    )
                     nc.vector.tensor_scalar(
-                        unmasked[:, BY_SCALAR:UNIT], c_row[q][:, half * BY_VECTOR : (half + 1) * BY_VECTOR],
+                        runs_of(unmasked[:, 0:width], PIECE)[:, :, BY_SCALAR:PIECE],
+                        runs_of(c_row[q][:, first * BY_VECTOR : (first + pieces) * BY_VECTOR], BY_VECTOR),
                         e_col[q][:, tb : tb + 1], b_col[q][:, tb : tb + 1], ALU.mult, ALU.max,
                     )
-                    weights = weights_of_sum.tile([P, UNIT], BF16, name="weights")
-                    nc.vector.tensor_tensor(weights[:], unmasked[:], adj[tb][:, cols], ALU.mult)
+                    weights = weights_of_sum.tile([P, 2 * PIECE], BF16, name="weights")
+                    nc.vector.tensor_tensor(
+                        weights[:, 0:width], unmasked[:, 0:width], adj[tb][:, first * PIECE : first * PIECE + width], ALU.mult
+                    )
                     tiles.append(weights)
                 return tiles
 
-            def sum_pair(unit, tiles, pair):
-                q = unit // 2
-                sums = psum_sums.tile([P, 2 * SUMS], F32, name="sums", bufs=4)
+            def prepare(unit):
+                q, first, pieces = unit
+                if first == 0:
+                    score_columns(q)
+                for c in range(first, first + pieces):
+                    score_rows(q, c)
+                tiles = make_weights(q, first, pieces)
+                if first == 0:
+                    flip_head(q)
+                return tiles
+
+            def sum_pair(q, tiles, pair):
+                sums = psum_sums.tile([P, 2 * SUMS], F32, name="sums", bufs=3)
                 for k in range(2):
                     jb = 2 * pair + k
                     for tb in range(BLOCKS):
@@ -170,7 +197,7 @@ def tile_multiheadgraphchannelattention_b_kernel(tc, table, w, a_src, a_dst, adj
 
             def divide_and_flip(sums, y_t, pair):
                 recip = ring.tile([P, 2], F32, name="recip", bufs=4)
-                nc.vector.reciprocal(recip[:].unsqueeze(2), sums.rearrange("p (k c) -> p k c", c=SUMS)[:, :, O : O + 1])
+                nc.vector.reciprocal(recip[:].unsqueeze(2), runs_of(sums, SUMS)[:, :, O : O + 1])
                 y = ring.tile([P, 2 * O], F32, name="y", bufs=3)
                 for k in range(2):
                     nc.scalar.activation(
@@ -180,31 +207,29 @@ def tile_multiheadgraphchannelattention_b_kernel(tc, table, w, a_src, a_dst, adj
                     at = (2 * (pair % 2) + k) * P
                     nc.tensor.transpose(y_t[:, at : at + P], y[:, k * O : (k + 1) * O], ident_f[:])
 
-            def elu_and_store(unit, y_t, half):
-                q, first = unit // 2, (unit % 2) * UNIT + half * 4 * P
-                e = ring.tile([O, 4 * P], F32, name="e")
+            def elu_and_store(q, c, y_t):
+                e = ring.tile([O, PIECE], F32, name="e")
                 nc.scalar.activation(e[:], y_t[:], FUNC.Relu, scale=-1.0)
                 nc.scalar.activation(e[:], e[:], FUNC.Exp, scale=-1.0)
-                result = ring.tile([O, 4 * P], F32, name="result")
+                result = ring.tile([O, PIECE], F32, name="result")
                 nc.vector.scalar_tensor_tensor(result[:], e[:], -1.0, y_t[:], ALU.add, ALU.max)
-                nc.sync.dma_start(out[q * O : (q + 1) * O, first : first + 4 * P], result[:])
+                nc.sync.dma_start(out[q * O : (q + 1) * O, c * PIECE : (c + 1) * PIECE], result[:])
 
             def sum_unit(unit, tiles):
+                q, first, pieces = unit
                 waiting = None
                 y_t = None
-                for pair in range(UNIT // (2 * P) + 1):
-                    sums = sum_pair(unit, tiles, pair) if pair < UNIT // (2 * P) else None
+                for pair in range(2 * pieces + 1):
+                    sums = sum_pair(q, tiles, pair) if pair < 2 * pieces else None
                     if waiting is not None:
                         if (pair - 1) % 2 == 0:
-                            y_t = psum_sums.tile([O, 4 * P], F32, name="y_t")
+                            y_t = psum_sums.tile([O, PIECE], F32, name="y_t")
                         divide_and_flip(waiting, y_t, pair - 1)
                         if (pair - 1) % 2 == 1:
-                            elu_and_store(unit, y_t, (pair - 1) // 2)
+                            elu_and_store(q, first + (pair - 1) // 2, y_t)
                     waiting = sums
 
-            units = H * N // UNIT
-            made = make_weights(0)
-            for unit in range(units):
-                ahead = make_weights(unit + 1) if unit + 1 < units else None
-                sum_unit(unit, made)
-                made = ahead
+            made = prepare(UNITS[0])
+            for i in range(len(UNITS)):
+                sum_unit(UNITS[i], made)
+                made = prepare(UNITS[i + 1]) if i + 1 < len(UNITS) else None

@@ -15,7 +15,7 @@ PIECES = N // PIECE
 BLOCKS = N // P
 NODES_A_ROW = 8
 CHUNKS = S // (P * NODES_A_ROW)
-BY_SCALAR = 144
+BY_SCALAR = 96
 BY_VECTOR = PIECE - BY_SCALAR
 ROW = 136
 SUMS = 130
@@ -74,7 +74,7 @@ def tile_multiheadgraphchannelattention_b_kernel(tc, table, w, a_src, a_dst, adj
 
         table_t = held.tile([D, S], BF16, name="table_t")
         hf = [held.tile([O, N], BF16, name=f"hf{q}") for q in range(H)]
-        c_row = [held.tile([P, PIECES * BY_VECTOR], F32, name=f"c_row{q}") for q in range(H)]
+        c_row = [held.tile([P, PIECES * BY_VECTOR], BF16, name=f"c_row{q}") for q in range(H)]
         s_row = [held.tile([P, PIECES * BY_SCALAR], F32, name=f"s_row{q}") for q in range(H)]
         b_col = [held.tile([P, BLOCKS], F32, name=f"b_col{q}") for q in range(H)]
         e_col = [held.tile([P, BLOCKS], F32, name=f"e_col{q}") for q in range(H)]

@@ -15,11 +15,11 @@ PIECES = N // PIECE
 BLOCKS = N // P
 NODES_A_ROW = 8
 CHUNKS = S // (P * NODES_A_ROW)
-BY_SCALAR = 96
-BY_VECTOR = PIECE - BY_SCALAR
-ROW = 136
-SUMS = 130
+ROW = 144
+SUMS = O + 2
 UNITS = [(q, c, 2) for q in range(H) for c in (0, 2)][:-1] + [(H - 1, 2, 1), (H - 1, 3, 1)]
+BANKS = 4
+HALF = PIECE // 2
 
 FLOPS = 2 * D * H * O * N + 2 * 2 * H * O * N + 2 * H * N * N * (O + 1)
 
@@ -35,6 +35,7 @@ def tile_multiheadgraphchannelattention_b_kernel(tc, table, w, a_src, a_dst, adj
         tc.tile_pool(name="held", bufs=1) as held,
         tc.tile_pool(name="ring", bufs=2) as ring,
         tc.tile_pool(name="weights_of_sum", bufs=2 * BLOCKS) as weights_of_sum,
+        tc.psum_pool(name="psum", bufs=2) as psum,
     ):
         offsets = lists.tile([P, N // 16], U16, name="offsets")
         nc.sync.dma_start(offsets[:], offs)
@@ -70,166 +71,152 @@ def tile_multiheadgraphchannelattention_b_kernel(tc, table, w, a_src, a_dst, adj
         for q in range(H):
             blocks_t = held.tile([P, BLOCKS * ROW], BF16, name=f"hf_t{q}")
             nc.gpsimd.memset(blocks_t[:], 1.0)
+            nc.gpsimd.memset(runs_of(blocks_t, ROW)[:, :, O + 1 : O + 2], -1.0)
             hf_t.append(blocks_t)
 
         table_t = held.tile([D, S], BF16, name="table_t")
         hf = [held.tile([O, N], BF16, name=f"hf{q}") for q in range(H)]
-        c_row = [held.tile([P, PIECES * BY_VECTOR], BF16, name=f"c_row{q}") for q in range(H)]
-        s_row = [held.tile([P, PIECES * BY_SCALAR], F32, name=f"s_row{q}") for q in range(H)]
+        c_row = [held.tile([P, N], BF16, name=f"c_row{q}") for q in range(H)]
         b_col = [held.tile([P, BLOCKS], F32, name=f"b_col{q}") for q in range(H)]
         e_col = [held.tile([P, BLOCKS], F32, name=f"e_col{q}") for q in range(H)]
-        d_col = [held.tile([P, BLOCKS], F32, name=f"d_col{q}") for q in range(H)]
-        n_col = [held.tile([P, BLOCKS], F32, name=f"n_col{q}") for q in range(H)]
 
-        with tc.psum_pool(name="psum_first", bufs=2) as psum_first:
-            a_cols_ps = psum_first.tile([P, NODES_A_ROW * P], BF16, name="a_cols_ps", tag="flipped")
-            nc.tensor.transpose(a_cols_ps[:, 0 : 2 * H], a_rows[0 : 2 * H, :], ident_bf[0 : 2 * H, 0 : 2 * H])
-            a_cols = held.tile([O, 2 * H], BF16, name="a_cols")
-            nc.vector.tensor_copy(a_cols[:], a_cols_ps[:, 0 : 2 * H])
-            a_src_wide = held.tile([O, H * P], BF16, name="a_src_wide")
-            for q in range(H):
-                nc.vector.tensor_copy(a_src_wide[:, q * P : (q + 1) * P], a_cols[:, q : q + 1].to_broadcast([O, P]))
+        a_cols_ps = psum.tile([P, NODES_A_ROW * P], BF16, name="a_cols_ps", tag="flipped")
+        nc.tensor.transpose(a_cols_ps[:, 0 : 2 * H], a_rows[0 : 2 * H, :], ident_bf[0 : 2 * H, 0 : 2 * H])
+        a_cols = held.tile([O, 2 * H], BF16, name="a_cols")
+        nc.vector.tensor_copy(a_cols[:], a_cols_ps[:, 0 : 2 * H])
+        a_src_wide = held.tile([O, H * P], BF16, name="a_src_wide")
+        for q in range(H):
+            nc.vector.tensor_copy(a_src_wide[:, q * P : (q + 1) * P], a_cols[:, q : q + 1].to_broadcast([O, P]))
 
-            for c in range(CHUNKS):
-                flipped = psum_first.tile([P, NODES_A_ROW * P], BF16, name="flipped")
-                for r in range(NODES_A_ROW):
-                    nc.tensor.transpose(flipped[:, r * P : (r + 1) * P], raw_chunks[c][:, r, :], ident_bf[:])
-                in_order = flipped.rearrange("d (r p) -> d p r", p=P)
-                window_part = runs_of(table_t[:, c * NODES_A_ROW * P : (c + 1) * NODES_A_ROW * P], NODES_A_ROW)
-                if c % 2 == 0:
-                    nc.vector.tensor_copy(window_part, in_order)
+        for c in range(CHUNKS):
+            flipped = psum.tile([P, NODES_A_ROW * P], BF16, name="flipped")
+            for r in range(NODES_A_ROW):
+                nc.tensor.transpose(flipped[:, r * P : (r + 1) * P], raw_chunks[c][:, r, :], ident_bf[:])
+            in_order = flipped.rearrange("d (r p) -> d p r", p=P)
+            window_part = runs_of(table_t[:, c * NODES_A_ROW * P : (c + 1) * NODES_A_ROW * P], NODES_A_ROW)
+            if c % 2 == 0:
+                nc.vector.tensor_copy(window_part, in_order)
+            else:
+                nc.scalar.copy(window_part, in_order)
+
+        def look_up(q, with_vector):
+            for c in range(PIECES):
+                picked = table_t[:].indirect(offsets[:, c * (PIECE // 16) : (c + 1) * (PIECE // 16)])
+                product = psum.tile([O, PIECE], F32, name="product", tag="bank", bufs=BANKS)
+                nc.tensor.matmul(product[:], proj[:, q * O : (q + 1) * O], picked, start=True, stop=True)
+                if with_vector and c % 2 == 0:
+                    nc.vector.tensor_copy(hf[q][:, c * PIECE : (c + 1) * PIECE], product[:])
                 else:
-                    nc.scalar.copy(window_part, in_order)
+                    nc.scalar.copy(hf[q][:, c * PIECE : (c + 1) * PIECE], product[:])
 
-            for q in range(H):
-                for c in range(PIECES):
-                    picked = table_t[:].indirect(offsets[:, c * (PIECE // 16) : (c + 1) * (PIECE // 16)])
-                    product = psum_first.tile([O, PIECE], F32, name="product", bufs=6)
-                    nc.tensor.matmul(product[:], proj[:, q * O : (q + 1) * O], picked, start=True, stop=True)
-                    if c % 2 == 0:
-                        nc.vector.tensor_copy(hf[q][:, c * PIECE : (c + 1) * PIECE], product[:])
-                    else:
-                        nc.scalar.copy(hf[q][:, c * PIECE : (c + 1) * PIECE], product[:])
-
-        with tc.psum_pool(name="psum_sums", bufs=2) as psum_sums:
-
-            def score_columns(q):
-                s_dst = psum_sums.tile([P, BLOCKS], F32, name="s_dst", tag="score")
-                for tb in range(BLOCKS):
-                    nc.tensor.matmul(
-                        s_dst[:, tb : tb + 1], hf[q][:, tb * P : (tb + 1) * P], a_cols[:, H + q : H + q + 1],
-                        start=True, stop=True,
-                    )
-                nc.scalar.activation(b_col[q][:], s_dst[:], FUNC.Exp)
-                nc.scalar.activation(e_col[q][:], s_dst[:], FUNC.Exp, scale=SLOPE)
-                nc.scalar.copy(d_col[q][:], s_dst[:])
-                nc.scalar.mul(n_col[q][:], s_dst[:], SLOPE - 1.0)
-
-            def score_rows(q, c):
-                s_src = psum_sums.tile([P, PIECE], F32, name="s_src", tag="score")
+        def score_columns(q):
+            s_dst = psum.tile([P, BLOCKS], F32, name="s_dst", tag="bank", bufs=BANKS)
+            for tb in range(BLOCKS):
                 nc.tensor.matmul(
-                    s_src[:], a_src_wide[:, q * P : (q + 1) * P], hf[q][:, c * PIECE : (c + 1) * PIECE],
+                    s_dst[:, tb : tb + 1], hf[q][:, tb * P : (tb + 1) * P], a_cols[:, H + q : H + q + 1],
                     start=True, stop=True,
                 )
-                nc.scalar.copy(s_row[q][:, c * BY_SCALAR : (c + 1) * BY_SCALAR], s_src[:, 0:BY_SCALAR])
-                nc.scalar.activation(
-                    c_row[q][:, c * BY_VECTOR : (c + 1) * BY_VECTOR], s_src[:, BY_SCALAR:PIECE], FUNC.Exp, scale=SLOPE - 1.0
+            nc.scalar.activation(b_col[q][:], s_dst[:], FUNC.Exp)
+            nc.scalar.activation(e_col[q][:], s_dst[:], FUNC.Exp, scale=SLOPE)
+
+        def score_rows(q, c):
+            s_src = psum.tile([P, PIECE], F32, name="s_src", tag="bank", bufs=BANKS)
+            for h in range(2):
+                nc.tensor.matmul(
+                    s_src[:, h * HALF : (h + 1) * HALF], a_src_wide[:, q * P : (q + 1) * P],
+                    hf[q][:, c * PIECE + h * HALF : c * PIECE + (h + 1) * HALF], start=True, stop=True,
+                )
+            nc.scalar.activation(c_row[q][:, c * PIECE : (c + 1) * PIECE], s_src[:], FUNC.Exp, scale=SLOPE - 1.0)
+
+        def flip_head(q):
+            for half in range(2):
+                flipped = psum.tile([P, 8 * P], BF16, name="flipped")
+                for k in range(8):
+                    tb = 8 * half + k
+                    nc.tensor.transpose(flipped[:, k * P : (k + 1) * P], hf[q][:, tb * P : (tb + 1) * P], ident_bf[:])
+                nc.scalar.copy(runs_of(hf_t[q], ROW)[:, 8 * half : 8 * half + 8, 0:O], runs_of(flipped, P))
+
+        def make_weights(q, first, pieces):
+            width = pieces * PIECE
+            columns = slice(first * PIECE, first * PIECE + width)
+            tiles = []
+            for tb in range(BLOCKS):
+                unmasked = ring.tile([P, 2 * PIECE], BF16, name="unmasked", bufs=4)
+                nc.vector.tensor_scalar(
+                    unmasked[:, 0:width], c_row[q][:, columns], e_col[q][:, tb : tb + 1], b_col[q][:, tb : tb + 1],
+                    ALU.mult, ALU.max,
+                )
+                weights = weights_of_sum.tile([P, 2 * PIECE], BF16, name="weights")
+                nc.vector.tensor_tensor(weights[:, 0:width], unmasked[:, 0:width], adj[tb][:, columns], ALU.mult)
+                tiles.append(weights)
+            return tiles
+
+        def prepare_head(q):
+            score_columns(q)
+            for c in range(PIECES):
+                score_rows(q, c)
+            flip_head(q)
+
+        def sum_pair(q, tiles, pair):
+            sums = psum.tile([P, 2 * SUMS], F32, name="sums", tag="bank", bufs=BANKS)
+            for k in range(2):
+                jb = 2 * pair + k
+                for tb in range(BLOCKS):
+                    nc.tensor.matmul(
+                        sums[:, k * SUMS : (k + 1) * SUMS],
+                        tiles[tb][:, jb * P : (jb + 1) * P],
+                        hf_t[q][:, tb * ROW : tb * ROW + SUMS],
+                        start=(tb == 0), stop=(tb == BLOCKS - 1),
+                    )
+            return sums
+
+        def divide_and_flip(sums, y_t, pair):
+            recip = ring.tile([P, 2, 2], F32, name="recip", bufs=4)
+            nc.vector.reciprocal(recip[:], runs_of(sums, SUMS)[:, :, O : O + 2])
+            above = ring.tile([P, 2 * O], F32, name="above", bufs=3)
+            below = ring.tile([P, 2 * O], F32, name="below", bufs=3)
+            for k in range(2):
+                numerators = sums[:, k * SUMS : k * SUMS + O]
+                nc.scalar.activation(above[:, k * O : (k + 1) * O], numerators, FUNC.Relu, scale=recip[:, k, 0:1])
+                nc.scalar.activation(below[:, k * O : (k + 1) * O], numerators, FUNC.Relu, scale=recip[:, k, 1:2])
+            nc.scalar.activation(below[:], below[:], FUNC.Exp, scale=-1.0)
+            for k in range(2):
+                at = (2 * (pair % 2) + k) * P
+                nc.tensor.matmul(
+                    y_t[:, at : at + P], above[:, k * O : (k + 1) * O], ident_f[:], is_transpose=True, start=True, stop=False
+                )
+                nc.tensor.matmul(
+                    y_t[:, at : at + P], below[:, k * O : (k + 1) * O], ident_f[:], is_transpose=True, start=False, stop=True
                 )
 
-            def flip_head(q):
-                for half in range(2):
-                    flipped = psum_sums.tile([P, 8 * P], BF16, name="flipped", bufs=1)
-                    for k in range(8):
-                        tb = 8 * half + k
-                        nc.tensor.transpose(flipped[:, k * P : (k + 1) * P], hf[q][:, tb * P : (tb + 1) * P], ident_bf[:])
-                    nc.scalar.copy(runs_of(hf_t[q], ROW)[:, 8 * half : 8 * half + 8, 0:O], runs_of(flipped, P))
+        def elu_and_store(q, c, y_t):
+            result = ring.tile([O, PIECE], F32, name="result")
+            nc.scalar.activation(result[:], y_t[:], FUNC.Copy, bias=-1.0)
+            nc.sync.dma_start(out[q * O : (q + 1) * O, c * PIECE : (c + 1) * PIECE], result[:])
 
-            def make_weights(q, first, pieces):
-                width = pieces * PIECE
-                tiles = []
-                for tb in range(BLOCKS):
-                    unmasked = ring.tile([P, 2 * PIECE], BF16, name="unmasked", bufs=4)
-                    ramp = ring.tile([P, 2 * BY_SCALAR], F32, name="ramp", bufs=3)
-                    nc.scalar.activation(
-                        ramp[:, 0 : pieces * BY_SCALAR], s_row[q][:, first * BY_SCALAR : (first + pieces) * BY_SCALAR],
-                        FUNC.Relu, bias=n_col[q][:, tb : tb + 1], scale=SLOPE - 1.0,
-                    )
-                    nc.scalar.activation(
-                        runs_of(unmasked[:, 0:width], PIECE)[:, :, 0:BY_SCALAR],
-                        runs_of(ramp[:, 0 : pieces * BY_SCALAR], BY_SCALAR),
-                        FUNC.Exp, bias=d_col[q][:, tb : tb + 1],
-                    )
-                    nc.vector.tensor_scalar(
-                        runs_of(unmasked[:, 0:width], PIECE)[:, :, BY_SCALAR:PIECE],
-                        runs_of(c_row[q][:, first * BY_VECTOR : (first + pieces) * BY_VECTOR], BY_VECTOR),
-                        e_col[q][:, tb : tb + 1], b_col[q][:, tb : tb + 1], ALU.mult, ALU.max,
-                    )
-                    weights = weights_of_sum.tile([P, 2 * PIECE], BF16, name="weights")
-                    nc.vector.tensor_tensor(
-                        weights[:, 0:width], unmasked[:, 0:width], adj[tb][:, first * PIECE : first * PIECE + width], ALU.mult
-                    )
-                    tiles.append(weights)
-                return tiles
+        def sum_unit(unit, tiles):
+            q, first, pieces = unit
+            waiting = None
+            y_t = None
+            for pair in range(2 * pieces + 1):
+                sums = sum_pair(q, tiles, pair) if pair < 2 * pieces else None
+                if waiting is not None:
+                    if (pair - 1) % 2 == 0:
+                        y_t = psum.tile([O, PIECE], F32, name="y_t")
+                    divide_and_flip(waiting, y_t, pair - 1)
+                    if (pair - 1) % 2 == 1:
+                        elu_and_store(q, first + (pair - 1) // 2, y_t)
+                waiting = sums
 
-            def prepare(unit):
-                q, first, pieces = unit
-                if first == 0:
-                    score_columns(q)
-                for c in range(first, first + pieces):
-                    score_rows(q, c)
-                tiles = make_weights(q, first, pieces)
-                if first == 0:
-                    flip_head(q)
-                return tiles
+        look_up(0, with_vector=True)
+        prepare_head(0)
+        made = make_weights(*UNITS[0])
+        for q in range(1, H):
+            look_up(q, with_vector=False)
 
-            def sum_pair(q, tiles, pair):
-                sums = psum_sums.tile([P, 2 * SUMS], F32, name="sums", bufs=3)
-                for k in range(2):
-                    jb = 2 * pair + k
-                    for tb in range(BLOCKS):
-                        nc.tensor.matmul(
-                            sums[:, k * SUMS : k * SUMS + O + 1],
-                            tiles[tb][:, jb * P : (jb + 1) * P],
-                            hf_t[q][:, tb * ROW : tb * ROW + O + 1],
-                            start=(tb == 0), stop=(tb == BLOCKS - 1),
-                        )
-                return sums
-
-            def divide_and_flip(sums, y_t, pair):
-                recip = ring.tile([P, 2], F32, name="recip", bufs=4)
-                nc.vector.reciprocal(recip[:].unsqueeze(2), runs_of(sums, SUMS)[:, :, O : O + 1])
-                y = ring.tile([P, 2 * O], F32, name="y", bufs=3)
-                for k in range(2):
-                    nc.scalar.activation(
-                        y[:, k * O : (k + 1) * O], sums[:, k * SUMS : k * SUMS + O], FUNC.Copy, scale=recip[:, k : k + 1]
-                    )
-                for k in range(2):
-                    at = (2 * (pair % 2) + k) * P
-                    nc.tensor.transpose(y_t[:, at : at + P], y[:, k * O : (k + 1) * O], ident_f[:])
-
-            def elu_and_store(q, c, y_t):
-                e = ring.tile([O, PIECE], F32, name="e")
-                nc.scalar.activation(e[:], y_t[:], FUNC.Relu, scale=-1.0)
-                nc.scalar.activation(e[:], e[:], FUNC.Exp, scale=-1.0)
-                result = ring.tile([O, PIECE], F32, name="result")
-                nc.vector.scalar_tensor_tensor(result[:], e[:], -1.0, y_t[:], ALU.add, ALU.max)
-                nc.sync.dma_start(out[q * O : (q + 1) * O, c * PIECE : (c + 1) * PIECE], result[:])
-
-            def sum_unit(unit, tiles):
-                q, first, pieces = unit
-                waiting = None
-                y_t = None
-                for pair in range(2 * pieces + 1):
-                    sums = sum_pair(q, tiles, pair) if pair < 2 * pieces else None
-                    if waiting is not None:
-                        if (pair - 1) % 2 == 0:
-                            y_t = psum_sums.tile([O, PIECE], F32, name="y_t")
-                        divide_and_flip(waiting, y_t, pair - 1)
-                        if (pair - 1) % 2 == 1:
-                            elu_and_store(q, first + (pair - 1) // 2, y_t)
-                    waiting = sums
-
-            made = prepare(UNITS[0])
-            for i in range(len(UNITS)):
-                sum_unit(UNITS[i], made)
-                made = prepare(UNITS[i + 1]) if i + 1 < len(UNITS) else None
+        for i in range(len(UNITS)):
+            q, first, pieces = UNITS[i]
+            if first == 0 and q + 1 < H:
+                prepare_head(q + 1)
+            sum_unit(UNITS[i], made)
+            made = make_weights(*UNITS[i + 1]) if i + 1 < len(UNITS) else None

@@ -17,9 +17,12 @@ NODES_A_ROW = 8
 CHUNKS = S // (P * NODES_A_ROW)
 ROW = 144
 SUMS = O + 2
-UNITS = [(q, c, 2) for q in range(H) for c in (0, 2)][:-1] + [(H - 1, 2, 1), (H - 1, 3, 1)]
-BANKS = 4
+A_BANK = PIECE // SUMS
 HALF = PIECE // 2
+UNITS = [(q, c, 2) for q in range(H) for c in (0, 2)][:-1] + [(H - 1, 2, 1), (H - 1, 3, 1)]
+LARGE_RING = 6
+SMALL_RING = 2
+TILES_AHEAD = 24
 
 FLOPS = 2 * D * H * O * N + 2 * 2 * H * O * N + 2 * H * N * N * (O + 1)
 
@@ -34,8 +37,7 @@ def tile_multiheadgraphchannelattention_b_kernel(tc, table, w, a_src, a_dst, adj
         tc.tile_pool(name="lists", bufs=1) as lists,
         tc.tile_pool(name="held", bufs=1) as held,
         tc.tile_pool(name="ring", bufs=2) as ring,
-        tc.tile_pool(name="weights_of_sum", bufs=2 * BLOCKS) as weights_of_sum,
-        tc.psum_pool(name="psum", bufs=2) as psum,
+        tc.psum_pool(name="psum", bufs=SMALL_RING) as psum,
     ):
         offsets = lists.tile([P, N // 16], U16, name="offsets")
         nc.sync.dma_start(offsets[:], offs)
@@ -70,7 +72,7 @@ def tile_multiheadgraphchannelattention_b_kernel(tc, table, w, a_src, a_dst, adj
         hf_t = []
         for q in range(H):
             blocks_t = held.tile([P, BLOCKS * ROW], BF16, name=f"hf_t{q}")
-            nc.gpsimd.memset(blocks_t[:], 1.0)
+            nc.gpsimd.memset(runs_of(blocks_t, ROW)[:, :, O:ROW], 1.0)
             nc.gpsimd.memset(runs_of(blocks_t, ROW)[:, :, O + 1 : O + 2], -1.0)
             hf_t.append(blocks_t)
 
@@ -80,16 +82,22 @@ def tile_multiheadgraphchannelattention_b_kernel(tc, table, w, a_src, a_dst, adj
         b_col = [held.tile([P, BLOCKS], F32, name=f"b_col{q}") for q in range(H)]
         e_col = [held.tile([P, BLOCKS], F32, name=f"e_col{q}") for q in range(H)]
 
-        a_cols_ps = psum.tile([P, NODES_A_ROW * P], BF16, name="a_cols_ps", tag="flipped")
-        nc.tensor.transpose(a_cols_ps[:, 0 : 2 * H], a_rows[0 : 2 * H, :], ident_bf[0 : 2 * H, 0 : 2 * H])
+        def large_bank(shape, dtype, name):
+            return psum.tile(shape, dtype, name=name, tag="large", bufs=LARGE_RING)
+
+        def small_bank(shape, dtype, name):
+            return psum.tile(shape, dtype, name=name, tag="small", bufs=SMALL_RING)
+
+        a_cols_ps = small_bank([P, 2 * H], BF16, "a_cols_ps")
+        nc.tensor.transpose(a_cols_ps[:], a_rows[0 : 2 * H, :], ident_bf[0 : 2 * H, 0 : 2 * H])
         a_cols = held.tile([O, 2 * H], BF16, name="a_cols")
-        nc.vector.tensor_copy(a_cols[:], a_cols_ps[:, 0 : 2 * H])
+        nc.vector.tensor_copy(a_cols[:], a_cols_ps[:])
         a_src_wide = held.tile([O, H * P], BF16, name="a_src_wide")
         for q in range(H):
             nc.vector.tensor_copy(a_src_wide[:, q * P : (q + 1) * P], a_cols[:, q : q + 1].to_broadcast([O, P]))
 
         for c in range(CHUNKS):
-            flipped = psum.tile([P, NODES_A_ROW * P], BF16, name="flipped")
+            flipped = large_bank([P, NODES_A_ROW * P], BF16, "flipped_chunk")
             for r in range(NODES_A_ROW):
                 nc.tensor.transpose(flipped[:, r * P : (r + 1) * P], raw_chunks[c][:, r, :], ident_bf[:])
             in_order = flipped.rearrange("d (r p) -> d p r", p=P)
@@ -102,15 +110,15 @@ def tile_multiheadgraphchannelattention_b_kernel(tc, table, w, a_src, a_dst, adj
         def look_up(q, with_vector):
             for c in range(PIECES):
                 picked = table_t[:].indirect(offsets[:, c * (PIECE // 16) : (c + 1) * (PIECE // 16)])
-                product = psum.tile([O, PIECE], F32, name="product", tag="bank", bufs=BANKS)
+                product = large_bank([O, PIECE], F32, "product")
                 nc.tensor.matmul(product[:], proj[:, q * O : (q + 1) * O], picked, start=True, stop=True)
                 if with_vector and c % 2 == 0:
                     nc.vector.tensor_copy(hf[q][:, c * PIECE : (c + 1) * PIECE], product[:])
                 else:
                     nc.scalar.copy(hf[q][:, c * PIECE : (c + 1) * PIECE], product[:])
 
-        def score_columns(q):
-            s_dst = psum.tile([P, BLOCKS], F32, name="s_dst", tag="bank", bufs=BANKS)
+        def score_columns(q, bank):
+            s_dst = bank([P, BLOCKS], F32, "s_dst")
             for tb in range(BLOCKS):
                 nc.tensor.matmul(
                     s_dst[:, tb : tb + 1], hf[q][:, tb * P : (tb + 1) * P], a_cols[:, H + q : H + q + 1],
@@ -119,8 +127,8 @@ def tile_multiheadgraphchannelattention_b_kernel(tc, table, w, a_src, a_dst, adj
             nc.scalar.activation(b_col[q][:], s_dst[:], FUNC.Exp)
             nc.scalar.activation(e_col[q][:], s_dst[:], FUNC.Exp, scale=SLOPE)
 
-        def score_rows(q, c):
-            s_src = psum.tile([P, PIECE], F32, name="s_src", tag="bank", bufs=BANKS)
+        def score_rows(q, c, bank):
+            s_src = bank([P, PIECE], F32, "s_src")
             for h in range(2):
                 nc.tensor.matmul(
                     s_src[:, h * HALF : (h + 1) * HALF], a_src_wide[:, q * P : (q + 1) * P],
@@ -130,93 +138,76 @@ def tile_multiheadgraphchannelattention_b_kernel(tc, table, w, a_src, a_dst, adj
 
         def flip_head(q):
             for half in range(2):
-                flipped = psum.tile([P, 8 * P], BF16, name="flipped")
+                flipped = small_bank([P, 8 * P], BF16, "flipped")
                 for k in range(8):
                     tb = 8 * half + k
                     nc.tensor.transpose(flipped[:, k * P : (k + 1) * P], hf[q][:, tb * P : (tb + 1) * P], ident_bf[:])
                 nc.scalar.copy(runs_of(hf_t[q], ROW)[:, 8 * half : 8 * half + 8, 0:O], runs_of(flipped, P))
 
-        def make_weights(q, first, pieces):
+        def prepare_head(q, bank):
+            score_columns(q, bank)
+            for c in range(PIECES):
+                score_rows(q, c, bank)
+            flip_head(q)
+
+        def make_and_sum(q, first, pieces):
             width = pieces * PIECE
             columns = slice(first * PIECE, first * PIECE + width)
-            tiles = []
+            blocks = width // P
+            banks = [large_bank([P, A_BANK * SUMS], F32, "sums") for b in range(0, blocks, A_BANK)]
             for tb in range(BLOCKS):
                 unmasked = ring.tile([P, 2 * PIECE], BF16, name="unmasked", bufs=4)
                 nc.vector.tensor_scalar(
                     unmasked[:, 0:width], c_row[q][:, columns], e_col[q][:, tb : tb + 1], b_col[q][:, tb : tb + 1],
                     ALU.mult, ALU.max,
                 )
-                weights = weights_of_sum.tile([P, 2 * PIECE], BF16, name="weights")
+                weights = ring.tile([P, 2 * PIECE], BF16, name="weights", bufs=TILES_AHEAD)
                 nc.vector.tensor_tensor(weights[:, 0:width], unmasked[:, 0:width], adj[tb][:, columns], ALU.mult)
-                tiles.append(weights)
-            return tiles
-
-        def prepare_head(q):
-            score_columns(q)
-            for c in range(PIECES):
-                score_rows(q, c)
-            flip_head(q)
-
-        def sum_pair(q, tiles, pair):
-            sums = psum.tile([P, 2 * SUMS], F32, name="sums", tag="bank", bufs=BANKS)
-            for k in range(2):
-                jb = 2 * pair + k
-                for tb in range(BLOCKS):
+                for jb in range(blocks):
+                    k = jb % A_BANK
                     nc.tensor.matmul(
-                        sums[:, k * SUMS : (k + 1) * SUMS],
-                        tiles[tb][:, jb * P : (jb + 1) * P],
+                        banks[jb // A_BANK][:, k * SUMS : (k + 1) * SUMS],
+                        weights[:, jb * P : (jb + 1) * P],
                         hf_t[q][:, tb * ROW : tb * ROW + SUMS],
-                        start=(tb == 0), stop=(tb == BLOCKS - 1),
+                        start=(tb == 0 and k == 0),
+                        stop=(tb == BLOCKS - 1 and (k == A_BANK - 1 or jb == blocks - 1)),
                     )
-            return sums
+            return banks
 
-        def divide_and_flip(sums, y_t, pair):
-            recip = ring.tile([P, 2, 2], F32, name="recip", bufs=4)
-            nc.vector.reciprocal(recip[:], runs_of(sums, SUMS)[:, :, O : O + 2])
-            above = ring.tile([P, 2 * O], F32, name="above", bufs=3)
-            below = ring.tile([P, 2 * O], F32, name="below", bufs=3)
-            for k in range(2):
+        def divide(sums, blocks):
+            recip = ring.tile([P, A_BANK, 2], F32, name="recip", bufs=6)
+            nc.vector.reciprocal(recip[:, 0:blocks, :], runs_of(sums[:, 0 : blocks * SUMS], SUMS)[:, :, O : O + 2])
+            above = ring.tile([P, A_BANK * O], F32, name="above", bufs=6)
+            below = ring.tile([P, A_BANK * O], F32, name="below", bufs=6)
+            for k in range(blocks):
                 numerators = sums[:, k * SUMS : k * SUMS + O]
                 nc.scalar.activation(above[:, k * O : (k + 1) * O], numerators, FUNC.Relu, scale=recip[:, k, 0:1])
                 nc.scalar.activation(below[:, k * O : (k + 1) * O], numerators, FUNC.Relu, scale=recip[:, k, 1:2])
-            nc.scalar.activation(below[:], below[:], FUNC.Exp, scale=-1.0)
-            for k in range(2):
-                at = (2 * (pair % 2) + k) * P
-                nc.tensor.matmul(
-                    y_t[:, at : at + P], above[:, k * O : (k + 1) * O], ident_f[:], is_transpose=True, start=True, stop=False
-                )
-                nc.tensor.matmul(
-                    y_t[:, at : at + P], below[:, k * O : (k + 1) * O], ident_f[:], is_transpose=True, start=False, stop=True
-                )
+            nc.scalar.activation(below[:, 0 : blocks * O], below[:, 0 : blocks * O], FUNC.Exp, scale=-1.0)
+            return [(above[:, k * O : (k + 1) * O], below[:, k * O : (k + 1) * O]) for k in range(blocks)]
 
-        def elu_and_store(q, c, y_t):
-            result = ring.tile([O, PIECE], F32, name="result")
-            nc.scalar.activation(result[:], y_t[:], FUNC.Copy, bias=-1.0)
-            nc.sync.dma_start(out[q * O : (q + 1) * O, c * PIECE : (c + 1) * PIECE], result[:])
-
-        def sum_unit(unit, tiles):
-            q, first, pieces = unit
-            waiting = None
-            y_t = None
-            for pair in range(2 * pieces + 1):
-                sums = sum_pair(q, tiles, pair) if pair < 2 * pieces else None
-                if waiting is not None:
-                    if (pair - 1) % 2 == 0:
-                        y_t = psum.tile([O, PIECE], F32, name="y_t")
-                    divide_and_flip(waiting, y_t, pair - 1)
-                    if (pair - 1) % 2 == 1:
-                        elu_and_store(q, first + (pair - 1) // 2, y_t)
-                waiting = sums
+        def finish(q, first, pieces, banks):
+            blocks = pieces * PIECE // P
+            halves = []
+            for b in range(len(banks)):
+                halves.extend(divide(banks[b], min(A_BANK, blocks - b * A_BANK)))
+            for c in range(pieces):
+                y_t = small_bank([O, PIECE], F32, "y_t")
+                for k in range(PIECE // P):
+                    above, below = halves[c * (PIECE // P) + k]
+                    nc.tensor.matmul(y_t[:, k * P : (k + 1) * P], above, ident_f[:], is_transpose=True, start=True, stop=False)
+                    nc.tensor.matmul(y_t[:, k * P : (k + 1) * P], below, ident_f[:], is_transpose=True, start=False, stop=True)
+                result = ring.tile([O, PIECE], F32, name="result")
+                nc.scalar.activation(result[:], y_t[:], FUNC.Copy, bias=-1.0)
+                nc.sync.dma_start(out[q * O : (q + 1) * O, (first + c) * PIECE : (first + c + 1) * PIECE], result[:])
 
         look_up(0, with_vector=True)
-        prepare_head(0)
-        made = make_weights(*UNITS[0])
+        prepare_head(0, large_bank)
         for q in range(1, H):
             look_up(q, with_vector=False)
 
-        for i in range(len(UNITS)):
-            q, first, pieces = UNITS[i]
+        for q, first, pieces in UNITS:
+            banks = make_and_sum(q, first, pieces)
+            finish(q, first, pieces, banks)
             if first == 0 and q + 1 < H:
-                prepare_head(q + 1)
-            sum_unit(UNITS[i], made)
-            made = make_weights(*UNITS[i + 1]) if i + 1 < len(UNITS) else None
+                prepare_head(q + 1, small_bank)

@@ -93,8 +93,11 @@ def tile_multiheadgraphchannelattention_b_kernel(tc, table, w, a_src, a_dst, adj
         a_cols = held.tile([O, 2 * H], BF16, name="a_cols")
         nc.vector.tensor_copy(a_cols[:], a_cols_ps[:])
         a_src_wide = held.tile([O, H * P], BF16, name="a_src_wide")
+        turn = [held.tile([O, P + 1], BF16, name=f"turn{q}") for q in range(H)]
         for q in range(H):
             nc.vector.tensor_copy(a_src_wide[:, q * P : (q + 1) * P], a_cols[:, q : q + 1].to_broadcast([O, P]))
+            nc.vector.tensor_copy(turn[q][:, 0:P], ident_bf[:])
+            nc.vector.tensor_copy(turn[q][:, P : P + 1], a_cols[:, H + q : H + q + 1])
 
         for c in range(CHUNKS):
             flipped = large_bank([P, NODES_A_ROW * P], BF16, "flipped_chunk")
@@ -117,16 +120,6 @@ def tile_multiheadgraphchannelattention_b_kernel(tc, table, w, a_src, a_dst, adj
                 else:
                     nc.scalar.copy(hf[q][:, c * PIECE : (c + 1) * PIECE], product[:])
 
-        def score_columns(q, bank):
-            s_dst = bank([P, BLOCKS], F32, "s_dst")
-            for tb in range(BLOCKS):
-                nc.tensor.matmul(
-                    s_dst[:, tb : tb + 1], hf[q][:, tb * P : (tb + 1) * P], a_cols[:, H + q : H + q + 1],
-                    start=True, stop=True,
-                )
-            nc.scalar.activation(b_col[q][:], s_dst[:], FUNC.Exp)
-            nc.scalar.activation(e_col[q][:], s_dst[:], FUNC.Exp, scale=SLOPE)
-
         def score_rows(q, c, bank):
             s_src = bank([P, PIECE], F32, "s_src")
             for h in range(2):
@@ -136,19 +129,26 @@ def tile_multiheadgraphchannelattention_b_kernel(tc, table, w, a_src, a_dst, adj
                 )
             nc.scalar.activation(c_row[q][:, c * PIECE : (c + 1) * PIECE], s_src[:], FUNC.Exp, scale=SLOPE - 1.0)
 
-        def flip_head(q):
-            for half in range(2):
-                flipped = small_bank([P, 8 * P], BF16, "flipped")
-                for k in range(8):
-                    tb = 8 * half + k
-                    nc.tensor.transpose(flipped[:, k * P : (k + 1) * P], hf[q][:, tb * P : (tb + 1) * P], ident_bf[:])
-                nc.scalar.copy(runs_of(hf_t[q], ROW)[:, 8 * half : 8 * half + 8, 0:O], runs_of(flipped, P))
+        def turn_head(q, bank):
+            for tb in range(0, BLOCKS, A_BANK):
+                blocks = min(A_BANK, BLOCKS - tb)
+                turned = bank([P, A_BANK * SUMS], F32, "turned")
+                for k in range(blocks):
+                    nc.tensor.matmul(
+                        turned[:, k * SUMS : k * SUMS + P + 1], hf[q][:, (tb + k) * P : (tb + k + 1) * P], turn[q][:],
+                        start=True, stop=True,
+                    )
+                by_block = runs_of(turned[:, 0 : blocks * SUMS], SUMS)
+                nc.scalar.activation(b_col[q][:, tb : tb + blocks].unsqueeze(2), by_block[:, :, P : P + 1], FUNC.Exp)
+                nc.scalar.activation(
+                    e_col[q][:, tb : tb + blocks].unsqueeze(2), by_block[:, :, P : P + 1], FUNC.Exp, scale=SLOPE
+                )
+                nc.scalar.copy(runs_of(hf_t[q], ROW)[:, tb : tb + blocks, 0:O], by_block[:, :, 0:O])
 
         def prepare_head(q, bank):
-            score_columns(q, bank)
             for c in range(PIECES):
                 score_rows(q, c, bank)
-            flip_head(q)
+            turn_head(q, bank)
 
         def make_and_sum(q, first, pieces):
             width = pieces * PIECE

@@ -23,6 +23,8 @@ UNITS = [(q, c, 2) for q in range(H) for c in (0, 2)][:-1] + [(H - 1, 2, 1), (H 
 LARGE_RING = 6
 SMALL_RING = 2
 TILES_AHEAD = 24
+BY_SCALAR = (11, 15)
+UNMASKED_AHEAD = 6
 
 FLOPS = 2 * D * H * O * N + 2 * 2 * H * O * N + 2 * H * N * N * (O + 1)
 
@@ -81,6 +83,7 @@ def tile_multiheadgraphchannelattention_b_kernel(tc, table, w, a_src, a_dst, adj
         c_row = [held.tile([P, N], BF16, name=f"c_row{q}") for q in range(H)]
         b_col = [held.tile([P, BLOCKS], F32, name=f"b_col{q}") for q in range(H)]
         e_col = [held.tile([P, BLOCKS], F32, name=f"e_col{q}") for q in range(H)]
+        minus_b_col = [held.tile([P, BLOCKS], F32, name=f"minus_b_col{q}") for q in range(H)]
 
         def large_bank(shape, dtype, name):
             return psum.tile(shape, dtype, name=name, tag="large", bufs=LARGE_RING)
@@ -143,6 +146,7 @@ def tile_multiheadgraphchannelattention_b_kernel(tc, table, w, a_src, a_dst, adj
                 nc.scalar.activation(
                     e_col[q][:, tb : tb + blocks].unsqueeze(2), by_block[:, :, P : P + 1], FUNC.Exp, scale=SLOPE
                 )
+                nc.scalar.mul(minus_b_col[q][:, tb : tb + blocks], b_col[q][:, tb : tb + blocks], -1.0)
                 nc.scalar.copy(runs_of(hf_t[q], ROW)[:, tb : tb + blocks, 0:O], by_block[:, :, 0:O])
 
         def prepare_head(q, bank):
@@ -156,11 +160,21 @@ def tile_multiheadgraphchannelattention_b_kernel(tc, table, w, a_src, a_dst, adj
             blocks = width // P
             banks = [large_bank([P, A_BANK * SUMS], F32, "sums") for b in range(0, blocks, A_BANK)]
             for tb in range(BLOCKS):
-                unmasked = ring.tile([P, 2 * PIECE], BF16, name="unmasked", bufs=4)
-                nc.vector.tensor_scalar(
-                    unmasked[:, 0:width], c_row[q][:, columns], e_col[q][:, tb : tb + 1], b_col[q][:, tb : tb + 1],
-                    ALU.mult, ALU.max,
-                )
+                unmasked = ring.tile([P, 2 * PIECE], BF16, name="unmasked", bufs=UNMASKED_AHEAD)
+                if tb in BY_SCALAR:
+                    excess = ring.tile([P, 2 * PIECE], F32, name="excess")
+                    nc.scalar.activation(
+                        excess[:, 0:width], c_row[q][:, columns], FUNC.Relu,
+                        bias=minus_b_col[q][:, tb : tb + 1], scale=e_col[q][:, tb : tb + 1],
+                    )
+                    nc.scalar.activation(
+                        unmasked[:, 0:width], excess[:, 0:width], FUNC.Identity, bias=b_col[q][:, tb : tb + 1]
+                    )
+                else:
+                    nc.vector.tensor_scalar(
+                        unmasked[:, 0:width], c_row[q][:, columns], e_col[q][:, tb : tb + 1], b_col[q][:, tb : tb + 1],
+                        ALU.mult, ALU.max,
+                    )
                 weights = ring.tile([P, 2 * PIECE], BF16, name="weights", bufs=TILES_AHEAD)
                 nc.vector.tensor_tensor(weights[:, 0:width], unmasked[:, 0:width], adj[tb][:, columns], ALU.mult)
                 for jb in range(blocks):

@@ -188,31 +188,50 @@ def tile_multiheadgraphchannelattention_b_kernel(tc, table, w, a_src, a_dst, adj
                     )
             return banks
 
-        def divide(sums, blocks):
+        def divide(sums, blocks, halved):
             recip = ring.tile([P, A_BANK, 2], F32, name="recip", bufs=6)
             nc.vector.reciprocal(recip[:, 0:blocks, :], runs_of(sums[:, 0 : blocks * SUMS], SUMS)[:, :, O : O + 2])
             above = ring.tile([P, A_BANK * O], F32, name="above", bufs=6)
-            below = ring.tile([P, A_BANK * O], F32, name="below", bufs=6)
+            below = None
+            if halved > 0:
+                below = ring.tile([P, A_BANK * O], F32, name="below", bufs=6)
             for k in range(blocks):
                 numerators = sums[:, k * SUMS : k * SUMS + O]
-                nc.scalar.activation(above[:, k * O : (k + 1) * O], numerators, FUNC.Relu, scale=recip[:, k, 0:1])
-                nc.scalar.activation(below[:, k * O : (k + 1) * O], numerators, FUNC.Relu, scale=recip[:, k, 1:2])
-            nc.scalar.activation(below[:, 0 : blocks * O], below[:, 0 : blocks * O], FUNC.Exp, scale=-1.0)
-            return [(above[:, k * O : (k + 1) * O], below[:, k * O : (k + 1) * O]) for k in range(blocks)]
+                if k < halved:
+                    nc.scalar.activation(above[:, k * O : (k + 1) * O], numerators, FUNC.Relu, scale=recip[:, k, 0:1])
+                    nc.scalar.activation(below[:, k * O : (k + 1) * O], numerators, FUNC.Relu, scale=recip[:, k, 1:2])
+                else:
+                    nc.scalar.activation(above[:, k * O : (k + 1) * O], numerators, FUNC.Copy, scale=recip[:, k, 0:1])
+            if halved > 0:
+                nc.scalar.activation(below[:, 0 : halved * O], below[:, 0 : halved * O], FUNC.Exp, scale=-1.0)
+            return [
+                (above[:, k * O : (k + 1) * O], below[:, k * O : (k + 1) * O] if k < halved else None) for k in range(blocks)
+            ]
 
         def finish(q, first, pieces, banks):
             blocks = pieces * PIECE // P
-            halves = []
+            divided = []
             for b in range(len(banks)):
-                halves.extend(divide(banks[b], min(A_BANK, blocks - b * A_BANK)))
+                here = min(A_BANK, blocks - b * A_BANK)
+                divided.extend(divide(banks[b], here, max(0, min(here, PIECE // P - b * A_BANK))))
             for c in range(pieces):
                 y_t = small_bank([O, PIECE], F32, "y_t")
-                for k in range(PIECE // P):
-                    above, below = halves[c * (PIECE // P) + k]
-                    nc.tensor.matmul(y_t[:, k * P : (k + 1) * P], above, ident_f[:], is_transpose=True, start=True, stop=False)
-                    nc.tensor.matmul(y_t[:, k * P : (k + 1) * P], below, ident_f[:], is_transpose=True, start=False, stop=True)
                 result = ring.tile([O, PIECE], F32, name="result")
-                nc.scalar.activation(result[:], y_t[:], FUNC.Copy, bias=-1.0)
+                for k in range(PIECE // P):
+                    above, below = divided[c * (PIECE // P) + k]
+                    at = y_t[:, k * P : (k + 1) * P]
+                    if c == 0:
+                        nc.tensor.matmul(at, above, ident_f[:], is_transpose=True, start=True, stop=False)
+                        nc.tensor.matmul(at, below, ident_f[:], is_transpose=True, start=False, stop=True)
+                    else:
+                        nc.tensor.matmul(at, above, ident_f[:], is_transpose=True, start=True, stop=True)
+                if c == 0:
+                    nc.scalar.activation(result[:], y_t[:], FUNC.Copy, bias=-1.0)
+                else:
+                    e = ring.tile([O, PIECE], F32, name="e")
+                    nc.scalar.activation(e[:], y_t[:], FUNC.Relu, scale=-1.0)
+                    nc.scalar.activation(e[:], e[:], FUNC.Exp, scale=-1.0)
+                    nc.vector.scalar_tensor_tensor(result[:], e[:], -1.0, y_t[:], ALU.add, ALU.max)
                 nc.sync.dma_start(out[q * O : (q + 1) * O, (first + c) * PIECE : (first + c + 1) * PIECE], result[:])
 
         look_up(0, with_vector=True)

@@ -13,13 +13,15 @@ SLOPE = 0.2
 PIECE = 512
 PIECES = N // PIECE
 BLOCKS = N // P
-NODES_A_ROW = 8
+NODES_A_ROW = 4
 CHUNKS = S // (P * NODES_A_ROW)
 ROW = 144
 SUMS = O + 2
 A_BANK = PIECE // SUMS
 HALF = PIECE // 2
-UNITS = [(q, c, 2) for q in range(H) for c in (0, 2)][:-1] + [(H - 1, 2, 1), (H - 1, 3, 1)]
+WIDE = 8
+UNITS = [(q, b, WIDE) for q in range(H) for b in (0, WIDE)][:-1] + [(H - 1, 8, 3), (H - 1, 11, 3), (H - 1, 14, 2)]
+A_RESULT = PIECE // P
 LARGE_RING = 6
 SMALL_RING = 2
 TILES_AHEAD = 24
@@ -150,19 +152,21 @@ def tile_multiheadgraphchannelattention_b_kernel(tc, table, w, a_src, a_dst, adj
                 nc.scalar.copy(runs_of(hf_t[q], ROW)[:, tb : tb + blocks, 0:O], by_block[:, :, 0:O])
 
         def prepare_head(q, bank):
-            for c in range(PIECES):
+            of_first_unit = WIDE * P // PIECE
+            for c in range(of_first_unit):
                 score_rows(q, c, bank)
             turn_head(q, bank)
+            for c in range(of_first_unit, PIECES):
+                score_rows(q, c, bank)
 
-        def make_and_sum(q, first, pieces):
-            width = pieces * PIECE
-            columns = slice(first * PIECE, first * PIECE + width)
-            blocks = width // P
+        def make_and_sum(q, first, blocks):
+            width = blocks * P
+            columns = slice(first * P, first * P + width)
             banks = [large_bank([P, A_BANK * SUMS], F32, "sums") for b in range(0, blocks, A_BANK)]
             for tb in range(BLOCKS):
-                unmasked = ring.tile([P, 2 * PIECE], BF16, name="unmasked", bufs=UNMASKED_AHEAD)
+                unmasked = ring.tile([P, WIDE * P], BF16, name="unmasked", bufs=UNMASKED_AHEAD)
                 if tb in BY_SCALAR:
-                    excess = ring.tile([P, 2 * PIECE], F32, name="excess")
+                    excess = ring.tile([P, WIDE * P], F32, name="excess")
                     nc.scalar.activation(
                         excess[:, 0:width], c_row[q][:, columns], FUNC.Relu,
                         bias=minus_b_col[q][:, tb : tb + 1], scale=e_col[q][:, tb : tb + 1],
@@ -175,7 +179,7 @@ def tile_multiheadgraphchannelattention_b_kernel(tc, table, w, a_src, a_dst, adj
                         unmasked[:, 0:width], c_row[q][:, columns], e_col[q][:, tb : tb + 1], b_col[q][:, tb : tb + 1],
                         ALU.mult, ALU.max,
                     )
-                weights = ring.tile([P, 2 * PIECE], BF16, name="weights", bufs=TILES_AHEAD)
+                weights = ring.tile([P, WIDE * P], BF16, name="weights", bufs=TILES_AHEAD)
                 nc.vector.tensor_tensor(weights[:, 0:width], unmasked[:, 0:width], adj[tb][:, columns], ALU.mult)
                 for jb in range(blocks):
                     k = jb % A_BANK
@@ -208,39 +212,43 @@ def tile_multiheadgraphchannelattention_b_kernel(tc, table, w, a_src, a_dst, adj
                 (above[:, k * O : (k + 1) * O], below[:, k * O : (k + 1) * O] if k < halved else None) for k in range(blocks)
             ]
 
-        def finish(q, first, pieces, banks):
-            blocks = pieces * PIECE // P
+        def finish(q, first, blocks, banks):
             divided = []
             for b in range(len(banks)):
                 here = min(A_BANK, blocks - b * A_BANK)
-                divided.extend(divide(banks[b], here, max(0, min(here, PIECE // P - b * A_BANK))))
-            for c in range(pieces):
-                y_t = small_bank([O, PIECE], F32, "y_t")
+                divided.extend(divide(banks[b], here, max(0, min(here, A_RESULT - b * A_BANK))))
+            for done in range(0, blocks, A_RESULT):
+                together = min(A_RESULT, blocks - done)
+                y_t = small_bank([O, together * P], F32, "y_t")
                 result = ring.tile([O, PIECE], F32, name="result")
-                for k in range(PIECE // P):
-                    above, below = divided[c * (PIECE // P) + k]
+                for k in range(together):
+                    above, below = divided[done + k]
                     at = y_t[:, k * P : (k + 1) * P]
-                    if c == 0:
+                    if done == 0:
                         nc.tensor.matmul(at, above, ident_f[:], is_transpose=True, start=True, stop=False)
                         nc.tensor.matmul(at, below, ident_f[:], is_transpose=True, start=False, stop=True)
                     else:
                         nc.tensor.matmul(at, above, ident_f[:], is_transpose=True, start=True, stop=True)
-                if c == 0:
-                    nc.scalar.activation(result[:], y_t[:], FUNC.Copy, bias=-1.0)
+                if done == 0:
+                    nc.scalar.activation(result[:, 0 : together * P], y_t[:], FUNC.Copy, bias=-1.0)
                 else:
                     e = ring.tile([O, PIECE], F32, name="e")
-                    nc.scalar.activation(e[:], y_t[:], FUNC.Relu, scale=-1.0)
-                    nc.scalar.activation(e[:], e[:], FUNC.Exp, scale=-1.0)
-                    nc.vector.scalar_tensor_tensor(result[:], e[:], -1.0, y_t[:], ALU.add, ALU.max)
-                nc.sync.dma_start(out[q * O : (q + 1) * O, (first + c) * PIECE : (first + c + 1) * PIECE], result[:])
+                    nc.scalar.activation(e[:, 0 : together * P], y_t[:], FUNC.Relu, scale=-1.0)
+                    nc.scalar.activation(e[:, 0 : together * P], e[:, 0 : together * P], FUNC.Exp, scale=-1.0)
+                    nc.vector.scalar_tensor_tensor(
+                        result[:, 0 : together * P], e[:, 0 : together * P], -1.0, y_t[:], ALU.add, ALU.max
+                    )
+                nc.sync.dma_start(
+                    out[q * O : (q + 1) * O, (first + done) * P : (first + done + together) * P], result[:, 0 : together * P]
+                )
 
         look_up(0, with_vector=True)
         prepare_head(0, large_bank)
         for q in range(1, H):
             look_up(q, with_vector=False)
 
-        for q, first, pieces in UNITS:
-            banks = make_and_sum(q, first, pieces)
-            finish(q, first, pieces, banks)
+        for q, first, blocks in UNITS:
+            banks = make_and_sum(q, first, blocks)
+            finish(q, first, blocks, banks)
             if first == 0 and q + 1 < H:
                 prepare_head(q + 1, small_bank)

@@ -24,9 +24,11 @@ UNITS = [(q, b, WIDE) for q in range(H) for b in (0, WIDE)][:-1] + [(H - 1, 8, 3
 A_RESULT = PIECE // P
 LARGE_RING = 6
 SMALL_RING = 2
-TILES_AHEAD = 24
+PAIR = 2
+PAIRS = BLOCKS // PAIR
+PAIRS_AHEAD = 12
 BY_SCALAR = (11, 15)
-UNMASKED_AHEAD = 6
+UNMASKED_AHEAD = 3
 
 FLOPS = 2 * D * H * O * N + 2 * 2 * H * O * N + 2 * H * N * N * (O + 1)
 
@@ -63,9 +65,10 @@ def tile_multiheadgraphchannelattention_b_kernel(tc, table, w, a_src, a_dst, adj
         nc.scalar.activation(warm[:], warm[:], FUNC.Exp)
 
         adj = []
-        for tb in range(BLOCKS):
-            adj_rows = held.tile([P, N], BF16, name=f"adj{tb}")
-            nc.sync.dma_start(adj_rows[:], adj_t[tb * P : (tb + 1) * P, :])
+        adj_pairs = adj_t.rearrange("(a k p) n -> a p k n", k=PAIR, p=P)
+        for a in range(PAIRS):
+            adj_rows = held.tile([P, PAIR, N], BF16, name=f"adj{a}")
+            nc.sync.dma_start(adj_rows[:], adj_pairs[a])
             adj.append(adj_rows)
 
         ident_bf = held.tile([P, P], BF16, name="ident_bf")
@@ -163,33 +166,37 @@ def tile_multiheadgraphchannelattention_b_kernel(tc, table, w, a_src, a_dst, adj
             width = blocks * P
             columns = slice(first * P, first * P + width)
             banks = [large_bank([P, A_BANK * SUMS], F32, "sums") for b in range(0, blocks, A_BANK)]
-            for tb in range(BLOCKS):
-                unmasked = ring.tile([P, WIDE * P], BF16, name="unmasked", bufs=UNMASKED_AHEAD)
-                if tb in BY_SCALAR:
-                    excess = ring.tile([P, WIDE * P], F32, name="excess")
-                    nc.scalar.activation(
-                        excess[:, 0:width], c_row[q][:, columns], FUNC.Relu,
-                        bias=minus_b_col[q][:, tb : tb + 1], scale=e_col[q][:, tb : tb + 1],
-                    )
-                    nc.scalar.activation(
-                        unmasked[:, 0:width], excess[:, 0:width], FUNC.Identity, bias=b_col[q][:, tb : tb + 1]
-                    )
-                else:
-                    nc.vector.tensor_scalar(
-                        unmasked[:, 0:width], c_row[q][:, columns], e_col[q][:, tb : tb + 1], b_col[q][:, tb : tb + 1],
-                        ALU.mult, ALU.max,
-                    )
-                weights = ring.tile([P, WIDE * P], BF16, name="weights", bufs=TILES_AHEAD)
-                nc.vector.tensor_tensor(weights[:, 0:width], unmasked[:, 0:width], adj[tb][:, columns], ALU.mult)
-                for jb in range(blocks):
-                    k = jb % A_BANK
-                    nc.tensor.matmul(
-                        banks[jb // A_BANK][:, k * SUMS : (k + 1) * SUMS],
-                        weights[:, jb * P : (jb + 1) * P],
-                        hf_t[q][:, tb * ROW : tb * ROW + SUMS],
-                        start=(tb == 0 and k == 0),
-                        stop=(tb == BLOCKS - 1 and (k == A_BANK - 1 or jb == blocks - 1)),
-                    )
+            for a in range(PAIRS):
+                unmasked = ring.tile([P, PAIR, WIDE * P], BF16, name="unmasked", bufs=UNMASKED_AHEAD)
+                for h in range(PAIR):
+                    tb = a * PAIR + h
+                    if tb in BY_SCALAR:
+                        excess = ring.tile([P, WIDE * P], F32, name="excess")
+                        nc.scalar.activation(
+                            excess[:, 0:width], c_row[q][:, columns], FUNC.Relu,
+                            bias=minus_b_col[q][:, tb : tb + 1], scale=e_col[q][:, tb : tb + 1],
+                        )
+                        nc.scalar.activation(
+                            unmasked[:, h, 0:width], excess[:, 0:width], FUNC.Identity, bias=b_col[q][:, tb : tb + 1]
+                        )
+                    else:
+                        nc.vector.tensor_scalar(
+                            unmasked[:, h, 0:width], c_row[q][:, columns], e_col[q][:, tb : tb + 1],
+                            b_col[q][:, tb : tb + 1], ALU.mult, ALU.max,
+                        )
+                weights = ring.tile([P, PAIR, WIDE * P], BF16, name="weights", bufs=PAIRS_AHEAD)
+                nc.vector.tensor_tensor(weights[:, :, 0:width], unmasked[:, :, 0:width], adj[a][:, :, columns], ALU.mult)
+                for h in range(PAIR):
+                    tb = a * PAIR + h
+                    for jb in range(blocks):
+                        k = jb % A_BANK
+                        nc.tensor.matmul(
+                            banks[jb // A_BANK][:, k * SUMS : (k + 1) * SUMS],
+                            weights[:, h, jb * P : (jb + 1) * P],
+                            hf_t[q][:, tb * ROW : tb * ROW + SUMS],
+                            start=(tb == 0 and k == 0),
+                            stop=(tb == BLOCKS - 1 and (k == A_BANK - 1 or jb == blocks - 1)),
+                        )
             return banks
 
         def divide(sums, blocks, halved):

@@ -1,3 +1,5 @@
+from functools import partial
+
 import concourse.mybir as mybir
 from concourse.masks import make_identity
 
@@ -26,9 +28,13 @@ LARGE_RING = 6
 SMALL_RING = 2
 PAIR = 2
 PAIRS = BLOCKS // PAIR
-PAIRS_AHEAD = 12
-BY_SCALAR = (11, 15)
-UNMASKED_AHEAD = 3
+PAIRS_AHEAD = 10
+BY_SCALAR = PAIRS - 1
+DIVIDE_BEHIND = 3
+FINISH_BEHIND = 4
+STORE_BEHIND = 7
+PREPARE_BEHIND = 6
+EXP_BEHIND = 2
 
 FLOPS = 2 * D * H * O * N + 2 * 2 * H * O * N + 2 * H * N * N * (O + 1)
 
@@ -101,11 +107,13 @@ def tile_multiheadgraphchannelattention_b_kernel(tc, table, w, a_src, a_dst, adj
         a_cols = held.tile([O, 2 * H], BF16, name="a_cols")
         nc.vector.tensor_copy(a_cols[:], a_cols_ps[:])
         a_src_wide = held.tile([O, H * P], BF16, name="a_src_wide")
-        turn = [held.tile([O, P + 1], BF16, name=f"turn{q}") for q in range(H)]
+        turn = [held.tile([O, SUMS], BF16, name=f"turn{q}") for q in range(H)]
+        s_cols = [held.tile([P, 2 * BLOCKS], F32, name=f"s_cols{q}") for q in range(H)]
         for q in range(H):
             nc.vector.tensor_copy(a_src_wide[:, q * P : (q + 1) * P], a_cols[:, q : q + 1].to_broadcast([O, P]))
             nc.vector.tensor_copy(turn[q][:, 0:P], ident_bf[:])
             nc.vector.tensor_copy(turn[q][:, P : P + 1], a_cols[:, H + q : H + q + 1])
+            nc.vector.tensor_copy(turn[q][:, P + 1 : P + 2], a_cols[:, q : q + 1])
 
         for c in range(CHUNKS):
             flipped = large_bank([P, NODES_A_ROW * P], BF16, "flipped_chunk")
@@ -123,7 +131,7 @@ def tile_multiheadgraphchannelattention_b_kernel(tc, table, w, a_src, a_dst, adj
                 picked = table_t[:].indirect(offsets[:, c * (PIECE // 16) : (c + 1) * (PIECE // 16)])
                 product = large_bank([O, PIECE], F32, "product")
                 nc.tensor.matmul(product[:], proj[:, q * O : (q + 1) * O], picked, start=True, stop=True)
-                if with_vector and c % 2 == 0:
+                if with_vector:
                     nc.vector.tensor_copy(hf[q][:, c * PIECE : (c + 1) * PIECE], product[:])
                 else:
                     nc.scalar.copy(hf[q][:, c * PIECE : (c + 1) * PIECE], product[:])
@@ -143,7 +151,7 @@ def tile_multiheadgraphchannelattention_b_kernel(tc, table, w, a_src, a_dst, adj
                 turned = bank([P, A_BANK * SUMS], F32, "turned")
                 for k in range(blocks):
                     nc.tensor.matmul(
-                        turned[:, k * SUMS : k * SUMS + P + 1], hf[q][:, (tb + k) * P : (tb + k + 1) * P], turn[q][:],
+                        turned[:, k * SUMS : (k + 1) * SUMS], hf[q][:, (tb + k) * P : (tb + k + 1) * P], turn[q][:],
                         start=True, stop=True,
                     )
                 by_block = runs_of(turned[:, 0 : blocks * SUMS], SUMS)
@@ -152,34 +160,72 @@ def tile_multiheadgraphchannelattention_b_kernel(tc, table, w, a_src, a_dst, adj
                     e_col[q][:, tb : tb + blocks].unsqueeze(2), by_block[:, :, P : P + 1], FUNC.Exp, scale=SLOPE
                 )
                 nc.scalar.mul(minus_b_col[q][:, tb : tb + blocks], b_col[q][:, tb : tb + blocks], -1.0)
+                if q > 0:
+                    for side, column in ((0, P + 1), (1, P)):
+                        nc.scalar.copy(
+                            s_cols[q][:, side * BLOCKS + tb : side * BLOCKS + tb + blocks].unsqueeze(2),
+                            by_block[:, :, column : column + 1],
+                        )
                 nc.scalar.copy(runs_of(hf_t[q], ROW)[:, tb : tb + blocks, 0:O], by_block[:, :, 0:O])
+
+        s_rows = {}
+
+        def spread_row(q, bank):
+            rows_ps = bank([2 * BLOCKS, P], F32, "rows_ps")
+            nc.tensor.transpose(rows_ps[:], s_cols[q][:], ident_f[:])
+            rows = ring.tile([2 * BLOCKS, P], F32, name="rows")
+            nc.scalar.copy(rows[:], rows_ps[:])
+            parked = (H - 1) * O + q
+            nc.sync.dma_start(out[parked, :].rearrange("(b p) -> b p", p=P), rows[0:BLOCKS, :])
+            s_rows[q] = []
+            for c in range(0, N, N // 2):
+                s_row = ring.tile([P, N // 2], F32, name="s_row")
+                nc.sync.dma_start(s_row[:], out[parked, c : c + N // 2].partition_broadcast(P))
+                s_rows[q].append(s_row)
+
+        def exp_row(q):
+            for h in range(2):
+                columns = slice(h * N // 2, (h + 1) * N // 2)
+                nc.scalar.activation(c_row[q][:, columns], s_rows[q][h][:], FUNC.Exp, scale=SLOPE - 1.0)
 
         def prepare_head(q, bank):
             of_first_unit = WIDE * P // PIECE
-            for c in range(of_first_unit):
-                score_rows(q, c, bank)
+            if q == 0:
+                for c in range(of_first_unit):
+                    score_rows(q, c, bank)
             turn_head(q, bank)
-            for c in range(of_first_unit, PIECES):
-                score_rows(q, c, bank)
+            if q == 0:
+                for c in range(of_first_unit, PIECES):
+                    score_rows(q, c, bank)
+            else:
+                spread_row(q, bank)
 
-        def make_and_sum(q, first, blocks):
+        def make_and_sum(q, first, blocks, by_scalar, steps):
             width = blocks * P
             columns = slice(first * P, first * P + width)
             banks = [large_bank([P, A_BANK * SUMS], F32, "sums") for b in range(0, blocks, A_BANK)]
-            for a in range(PAIRS):
-                unmasked = ring.tile([P, PAIR, WIDE * P], BF16, name="unmasked", bufs=UNMASKED_AHEAD)
+            if by_scalar:
+                from_scalar = ring.tile([P, PAIR, WIDE * P], BF16, name="from_scalar")
                 for h in range(PAIR):
-                    tb = a * PAIR + h
-                    if tb in BY_SCALAR:
-                        excess = ring.tile([P, WIDE * P], F32, name="excess")
-                        nc.scalar.activation(
-                            excess[:, 0:width], c_row[q][:, columns], FUNC.Relu,
-                            bias=minus_b_col[q][:, tb : tb + 1], scale=e_col[q][:, tb : tb + 1],
-                        )
-                        nc.scalar.activation(
-                            unmasked[:, h, 0:width], excess[:, 0:width], FUNC.Identity, bias=b_col[q][:, tb : tb + 1]
-                        )
-                    else:
+                    tb = BY_SCALAR * PAIR + h
+                    excess = ring.tile([P, WIDE * P], F32, name="excess")
+                    nc.scalar.activation(
+                        excess[:, 0:width], c_row[q][:, columns], FUNC.Relu,
+                        bias=minus_b_col[q][:, tb : tb + 1], scale=e_col[q][:, tb : tb + 1],
+                    )
+                    nc.scalar.activation(
+                        from_scalar[:, h, 0:width], excess[:, 0:width], FUNC.Identity, bias=b_col[q][:, tb : tb + 1]
+                    )
+            for a in range(PAIRS):
+                for behind, step in steps:
+                    if behind == a:
+                        step()
+                if by_scalar and a == BY_SCALAR:
+                    unmasked = from_scalar
+                else:
+                    unmasked = ring.tile([P, PAIR, WIDE * P], BF16, name="unmasked")
+                    for h in range(PAIR):
+                        tb = a * PAIR + h
                         nc.vector.tensor_scalar(
                             unmasked[:, h, 0:width], c_row[q][:, columns], e_col[q][:, tb : tb + 1],
                             b_col[q][:, tb : tb + 1], ALU.mult, ALU.max,
@@ -219,15 +265,18 @@ def tile_multiheadgraphchannelattention_b_kernel(tc, table, w, a_src, a_dst, adj
                 (above[:, k * O : (k + 1) * O], below[:, k * O : (k + 1) * O] if k < halved else None) for k in range(blocks)
             ]
 
-        def finish(q, first, blocks, banks):
-            divided = []
+        def divide_unit(blocks, banks, divided):
+            parts = []
             for b in range(len(banks)):
                 here = min(A_BANK, blocks - b * A_BANK)
-                divided.extend(divide(banks[b], here, max(0, min(here, A_RESULT - b * A_BANK))))
+                parts.extend(divide(banks[b], here, max(0, min(here, A_RESULT - b * A_BANK))))
+            divided.append(parts)
+
+        def finish(q, first, blocks, divided, results):
+            divided = divided[0]
             for done in range(0, blocks, A_RESULT):
                 together = min(A_RESULT, blocks - done)
                 y_t = small_bank([O, together * P], F32, "y_t")
-                result = ring.tile([O, PIECE], F32, name="result")
                 for k in range(together):
                     above, below = divided[done + k]
                     at = y_t[:, k * P : (k + 1) * P]
@@ -237,25 +286,46 @@ def tile_multiheadgraphchannelattention_b_kernel(tc, table, w, a_src, a_dst, adj
                     else:
                         nc.tensor.matmul(at, above, ident_f[:], is_transpose=True, start=True, stop=True)
                 if done == 0:
+                    result = ring.tile([O, PIECE], F32, name="result", bufs=3)
                     nc.scalar.activation(result[:, 0 : together * P], y_t[:], FUNC.Copy, bias=-1.0)
                 else:
                     e = ring.tile([O, PIECE], F32, name="e")
                     nc.scalar.activation(e[:, 0 : together * P], y_t[:], FUNC.Relu, scale=-1.0)
                     nc.scalar.activation(e[:, 0 : together * P], e[:, 0 : together * P], FUNC.Exp, scale=-1.0)
-                    nc.vector.scalar_tensor_tensor(
-                        result[:, 0 : together * P], e[:, 0 : together * P], -1.0, y_t[:], ALU.add, ALU.max
-                    )
+                    results.append((done, together, e, y_t))
+                    continue
+                nc.sync.dma_start(
+                    out[q * O : (q + 1) * O, (first + done) * P : (first + done + together) * P], result[:, 0 : together * P]
+                )
+
+        def store_rest(q, first, results):
+            for done, together, e, y_t in results:
+                result = ring.tile([O, PIECE], F32, name="result", bufs=3)
+                nc.vector.scalar_tensor_tensor(
+                    result[:, 0 : together * P], e[:, 0 : together * P], -1.0, y_t[:], ALU.add, ALU.max
+                )
                 nc.sync.dma_start(
                     out[q * O : (q + 1) * O, (first + done) * P : (first + done + together) * P], result[:, 0 : together * P]
                 )
 
         look_up(0, with_vector=True)
         prepare_head(0, large_bank)
-        for q in range(1, H):
+        for q in range(H - 1, 0, -1):
             look_up(q, with_vector=False)
 
-        for q, first, blocks in UNITS:
-            banks = make_and_sum(q, first, blocks)
-            finish(q, first, blocks, banks)
-            if first == 0 and q + 1 < H:
-                prepare_head(q + 1, small_bank)
+        waiting = []
+        for u, (q, first, blocks) in enumerate(UNITS):
+            if q + 1 < H:
+                if first == 0:
+                    waiting.append((PREPARE_BEHIND, partial(prepare_head, q + 1, small_bank)))
+                else:
+                    waiting.append((EXP_BEHIND, partial(exp_row, q + 1)))
+            banks = make_and_sum(q, first, blocks, u > 0, waiting)
+            divided, results = [], []
+            waiting = [
+                (DIVIDE_BEHIND, partial(divide_unit, blocks, banks, divided)),
+                (FINISH_BEHIND, partial(finish, q, first, blocks, divided, results)),
+                (STORE_BEHIND, partial(store_rest, q, first, results)),
+            ]
+        for behind, step in waiting:
+            step()

@@ -32,9 +32,9 @@ PAIRS_AHEAD = 10
 BY_SCALAR = PAIRS - 1
 DIVIDE_BEHIND = 3
 FINISH_BEHIND = 4
-STORE_BEHIND = 7
-PREPARE_BEHIND = 6
-EXP_BEHIND = 2
+END_BEHIND = 6
+TURN_BEHIND = 1
+EXP_BEHIND = 5
 
 FLOPS = 2 * D * H * O * N + 2 * 2 * H * O * N + 2 * H * N * N * (O + 1)
 
@@ -145,62 +145,48 @@ def tile_multiheadgraphchannelattention_b_kernel(tc, table, w, a_src, a_dst, adj
                 )
             nc.scalar.activation(c_row[q][:, c * PIECE : (c + 1) * PIECE], s_src[:], FUNC.Exp, scale=SLOPE - 1.0)
 
-        def turn_head(q, bank):
-            for tb in range(0, BLOCKS, A_BANK):
-                blocks = min(A_BANK, BLOCKS - tb)
-                turned = bank([P, A_BANK * SUMS], F32, "turned")
-                for k in range(blocks):
-                    nc.tensor.matmul(
-                        turned[:, k * SUMS : (k + 1) * SUMS], hf[q][:, (tb + k) * P : (tb + k + 1) * P], turn[q][:],
-                        start=True, stop=True,
-                    )
-                by_block = runs_of(turned[:, 0 : blocks * SUMS], SUMS)
-                nc.scalar.activation(b_col[q][:, tb : tb + blocks].unsqueeze(2), by_block[:, :, P : P + 1], FUNC.Exp)
-                nc.scalar.activation(
-                    e_col[q][:, tb : tb + blocks].unsqueeze(2), by_block[:, :, P : P + 1], FUNC.Exp, scale=SLOPE
+        def turn_blocks(q, tb, bank):
+            blocks = min(A_BANK, BLOCKS - tb)
+            turned = bank([P, A_BANK * SUMS], F32, "turned")
+            for k in range(blocks):
+                nc.tensor.matmul(
+                    turned[:, k * SUMS : (k + 1) * SUMS], hf[q][:, (tb + k) * P : (tb + k + 1) * P], turn[q][:],
+                    start=True, stop=True,
                 )
-                nc.scalar.mul(minus_b_col[q][:, tb : tb + blocks], b_col[q][:, tb : tb + blocks], -1.0)
-                if q > 0:
-                    for side, column in ((0, P + 1), (1, P)):
-                        nc.scalar.copy(
-                            s_cols[q][:, side * BLOCKS + tb : side * BLOCKS + tb + blocks].unsqueeze(2),
-                            by_block[:, :, column : column + 1],
-                        )
-                nc.scalar.copy(runs_of(hf_t[q], ROW)[:, tb : tb + blocks, 0:O], by_block[:, :, 0:O])
+            by_block = runs_of(turned[:, 0 : blocks * SUMS], SUMS)
+            nc.scalar.activation(b_col[q][:, tb : tb + blocks].unsqueeze(2), by_block[:, :, P : P + 1], FUNC.Exp)
+            nc.scalar.activation(
+                e_col[q][:, tb : tb + blocks].unsqueeze(2), by_block[:, :, P : P + 1], FUNC.Exp, scale=SLOPE
+            )
+            nc.scalar.mul(minus_b_col[q][:, tb : tb + blocks], b_col[q][:, tb : tb + blocks], -1.0)
+            if q > 0:
+                for side, column in ((0, P + 1), (1, P)):
+                    nc.scalar.copy(
+                        s_cols[q][:, side * BLOCKS + tb : side * BLOCKS + tb + blocks].unsqueeze(2),
+                        by_block[:, :, column : column + 1],
+                    )
+            nc.scalar.copy(runs_of(hf_t[q], ROW)[:, tb : tb + blocks, 0:O], by_block[:, :, 0:O])
 
         s_rows = {}
 
-        def spread_row(q, bank):
-            rows_ps = bank([2 * BLOCKS, P], F32, "rows_ps")
+        def spread_row(q):
+            rows_ps = small_bank([2 * BLOCKS, P], F32, "rows_ps")
             nc.tensor.transpose(rows_ps[:], s_cols[q][:], ident_f[:])
             rows = ring.tile([2 * BLOCKS, P], F32, name="rows")
             nc.scalar.copy(rows[:], rows_ps[:])
             parked = (H - 1) * O + q
             nc.sync.dma_start(out[parked, :].rearrange("(b p) -> b p", p=P), rows[0:BLOCKS, :])
-            s_rows[q] = []
-            for c in range(0, N, N // 2):
-                s_row = ring.tile([P, N // 2], F32, name="s_row")
-                nc.sync.dma_start(s_row[:], out[parked, c : c + N // 2].partition_broadcast(P))
-                s_rows[q].append(s_row)
-
-        def exp_row(q):
             for h in range(2):
-                columns = slice(h * N // 2, (h + 1) * N // 2)
-                nc.scalar.activation(c_row[q][:, columns], s_rows[q][h][:], FUNC.Exp, scale=SLOPE - 1.0)
+                s_row = ring.tile([P, N // 2], F32, name="s_row")
+                nc.sync.dma_start(s_row[:], out[parked, h * N // 2 : (h + 1) * N // 2].partition_broadcast(P))
+                s_rows[q, h] = s_row
 
-        def prepare_head(q, bank):
-            of_first_unit = WIDE * P // PIECE
-            if q == 0:
-                for c in range(of_first_unit):
-                    score_rows(q, c, bank)
-            turn_head(q, bank)
-            if q == 0:
-                for c in range(of_first_unit, PIECES):
-                    score_rows(q, c, bank)
-            else:
-                spread_row(q, bank)
+        def exp_row(q, h):
+            nc.scalar.activation(
+                c_row[q][:, h * N // 2 : (h + 1) * N // 2], s_rows[q, h][:], FUNC.Exp, scale=SLOPE - 1.0
+            )
 
-        def make_and_sum(q, first, blocks, by_scalar, steps):
+        def make_and_sum(q, first, blocks, by_scalar, agenda):
             width = blocks * P
             columns = slice(first * P, first * P + width)
             banks = [large_bank([P, A_BANK * SUMS], F32, "sums") for b in range(0, blocks, A_BANK)]
@@ -217,9 +203,8 @@ def tile_multiheadgraphchannelattention_b_kernel(tc, table, w, a_src, a_dst, adj
                         from_scalar[:, h, 0:width], excess[:, 0:width], FUNC.Identity, bias=b_col[q][:, tb : tb + 1]
                     )
             for a in range(PAIRS):
-                for behind, step in steps:
-                    if behind == a:
-                        step()
+                for step in agenda[a]:
+                    step()
                 if by_scalar and a == BY_SCALAR:
                     unmasked = from_scalar
                 else:
@@ -245,87 +230,91 @@ def tile_multiheadgraphchannelattention_b_kernel(tc, table, w, a_src, a_dst, adj
                         )
             return banks
 
-        def divide(sums, blocks, halved):
+        def divide(sums, blocks, by_vector):
             recip = ring.tile([P, A_BANK, 2], F32, name="recip", bufs=6)
             nc.vector.reciprocal(recip[:, 0:blocks, :], runs_of(sums[:, 0 : blocks * SUMS], SUMS)[:, :, O : O + 2])
             above = ring.tile([P, A_BANK * O], F32, name="above", bufs=6)
-            below = None
-            if halved > 0:
-                below = ring.tile([P, A_BANK * O], F32, name="below", bufs=6)
+            below = None if by_vector else ring.tile([P, A_BANK * O], F32, name="below", bufs=3)
             for k in range(blocks):
                 numerators = sums[:, k * SUMS : k * SUMS + O]
-                if k < halved:
+                if by_vector:
+                    nc.scalar.activation(above[:, k * O : (k + 1) * O], numerators, FUNC.Copy, scale=recip[:, k, 0:1])
+                else:
                     nc.scalar.activation(above[:, k * O : (k + 1) * O], numerators, FUNC.Relu, scale=recip[:, k, 0:1])
                     nc.scalar.activation(below[:, k * O : (k + 1) * O], numerators, FUNC.Relu, scale=recip[:, k, 1:2])
-                else:
-                    nc.scalar.activation(above[:, k * O : (k + 1) * O], numerators, FUNC.Copy, scale=recip[:, k, 0:1])
-            if halved > 0:
-                nc.scalar.activation(below[:, 0 : halved * O], below[:, 0 : halved * O], FUNC.Exp, scale=-1.0)
+            if not by_vector:
+                nc.scalar.activation(below[:, 0 : blocks * O], below[:, 0 : blocks * O], FUNC.Exp, scale=-1.0)
             return [
-                (above[:, k * O : (k + 1) * O], below[:, k * O : (k + 1) * O] if k < halved else None) for k in range(blocks)
+                (above[:, k * O : (k + 1) * O], None if by_vector else below[:, k * O : (k + 1) * O]) for k in range(blocks)
             ]
 
-        def divide_unit(blocks, banks, divided):
-            parts = []
+        def divide_unit(blocks, banks, by_vector, divided):
             for b in range(len(banks)):
-                here = min(A_BANK, blocks - b * A_BANK)
-                parts.extend(divide(banks[b], here, max(0, min(here, A_RESULT - b * A_BANK))))
-            divided.append(parts)
+                divided.extend(divide(banks[b], min(A_BANK, blocks - b * A_BANK), by_vector))
 
-        def finish(q, first, blocks, divided, results):
-            divided = divided[0]
-            for done in range(0, blocks, A_RESULT):
-                together = min(A_RESULT, blocks - done)
-                y_t = small_bank([O, together * P], F32, "y_t")
-                for k in range(together):
-                    above, below = divided[done + k]
-                    at = y_t[:, k * P : (k + 1) * P]
-                    if done == 0:
-                        nc.tensor.matmul(at, above, ident_f[:], is_transpose=True, start=True, stop=False)
-                        nc.tensor.matmul(at, below, ident_f[:], is_transpose=True, start=False, stop=True)
-                    else:
-                        nc.tensor.matmul(at, above, ident_f[:], is_transpose=True, start=True, stop=True)
-                if done == 0:
-                    result = ring.tile([O, PIECE], F32, name="result", bufs=3)
-                    nc.scalar.activation(result[:, 0 : together * P], y_t[:], FUNC.Copy, bias=-1.0)
-                else:
-                    e = ring.tile([O, PIECE], F32, name="e")
-                    nc.scalar.activation(e[:, 0 : together * P], y_t[:], FUNC.Relu, scale=-1.0)
-                    nc.scalar.activation(e[:, 0 : together * P], e[:, 0 : together * P], FUNC.Exp, scale=-1.0)
-                    results.append((done, together, e, y_t))
-                    continue
-                nc.sync.dma_start(
-                    out[q * O : (q + 1) * O, (first + done) * P : (first + done + together) * P], result[:, 0 : together * P]
-                )
+        def store(q, block, together, result):
+            nc.sync.dma_start(
+                out[q * O : (q + 1) * O, block * P : (block + together) * P], result[:, 0 : together * P]
+            )
 
-        def store_rest(q, first, results):
-            for done, together, e, y_t in results:
+        def turn_results(q, first, done, together, by_vector, divided, halfway):
+            y_t = small_bank([O, together * P], F32, "y_t")
+            for k in range(together):
+                above, below = divided[done + k]
+                at = y_t[:, k * P : (k + 1) * P]
+                nc.tensor.matmul(at, above, ident_f[:], is_transpose=True, start=True, stop=by_vector)
+                if not by_vector:
+                    nc.tensor.matmul(at, below, ident_f[:], is_transpose=True, start=False, stop=True)
+            if by_vector:
+                e = ring.tile([O, PIECE], F32, name="e")
+                nc.scalar.activation(e[:, 0 : together * P], y_t[:], FUNC.Relu, scale=-1.0)
+                nc.scalar.activation(e[:, 0 : together * P], e[:, 0 : together * P], FUNC.Exp, scale=-1.0)
+                halfway[done] = (e, y_t)
+            else:
                 result = ring.tile([O, PIECE], F32, name="result", bufs=3)
-                nc.vector.scalar_tensor_tensor(
-                    result[:, 0 : together * P], e[:, 0 : together * P], -1.0, y_t[:], ALU.add, ALU.max
-                )
-                nc.sync.dma_start(
-                    out[q * O : (q + 1) * O, (first + done) * P : (first + done + together) * P], result[:, 0 : together * P]
-                )
+                nc.scalar.activation(result[:, 0 : together * P], y_t[:], FUNC.Copy, bias=-1.0)
+                store(q, first + done, together, result)
+
+        def end_elu(q, first, done, together, halfway):
+            e, y_t = halfway[done]
+            result = ring.tile([O, PIECE], F32, name="result", bufs=3)
+            nc.vector.scalar_tensor_tensor(
+                result[:, 0 : together * P], e[:, 0 : together * P], -1.0, y_t[:], ALU.add, ALU.max
+            )
+            store(q, first + done, together, result)
 
         look_up(0, with_vector=True)
-        prepare_head(0, large_bank)
+        of_first_unit = WIDE * P // PIECE
+        for c in range(of_first_unit):
+            score_rows(0, c, large_bank)
+        for tb in range(0, BLOCKS, A_BANK):
+            turn_blocks(0, tb, large_bank)
+        for c in range(of_first_unit, PIECES):
+            score_rows(0, c, large_bank)
         for q in range(H - 1, 0, -1):
             look_up(q, with_vector=False)
 
-        waiting = []
+        agenda = {a: [] for a in range(PAIRS)}
         for u, (q, first, blocks) in enumerate(UNITS):
-            if q + 1 < H:
-                if first == 0:
-                    waiting.append((PREPARE_BEHIND, partial(prepare_head, q + 1, small_bank)))
-                else:
-                    waiting.append((EXP_BEHIND, partial(exp_row, q + 1)))
-            banks = make_and_sum(q, first, blocks, u > 0, waiting)
-            divided, results = [], []
-            waiting = [
-                (DIVIDE_BEHIND, partial(divide_unit, blocks, banks, divided)),
-                (FINISH_BEHIND, partial(finish, q, first, blocks, divided, results)),
-                (STORE_BEHIND, partial(store_rest, q, first, results)),
-            ]
-        for behind, step in waiting:
-            step()
+            if q + 1 < H and first == 0:
+                for tb in range(0, BLOCKS, A_BANK):
+                    agenda[TURN_BEHIND + tb // A_BANK].append(partial(turn_blocks, q + 1, tb, small_bank))
+                agenda[PAIRS - 1].append(partial(spread_row, q + 1))
+            elif q + 1 < H:
+                for h in range(2):
+                    agenda[EXP_BEHIND + h].append(partial(exp_row, q + 1, h))
+            banks = make_and_sum(q, first, blocks, u > 0, agenda)
+            by_vector = first == 0
+            divided, halfway = [], {}
+            agenda = {a: [] for a in range(PAIRS)}
+            agenda[DIVIDE_BEHIND].append(partial(divide_unit, blocks, banks, by_vector, divided))
+            for g, done in enumerate(range(0, blocks, A_RESULT)):
+                together = min(A_RESULT, blocks - done)
+                agenda[FINISH_BEHIND + g].append(
+                    partial(turn_results, q, first, done, together, by_vector, divided, halfway)
+                )
+                if by_vector:
+                    agenda[END_BEHIND + g].append(partial(end_elu, q, first, done, together, halfway))
+        for a in range(PAIRS):
+            for step in agenda[a]:
+                step()

@@ -18,8 +18,9 @@ BLOCKS = N // P
 NODES_A_ROW = 4
 CHUNKS = S // (P * NODES_A_ROW)
 ROW = 144
-SUMS = O + 2
-A_BANK = PIECE // SUMS
+SUMS = O + 1
+TURNED = O + 2
+A_BANK = PIECE // TURNED
 HALF = PIECE // 2
 WIDE = 8
 UNITS = [(q, b, WIDE) for q in range(H) for b in (0, WIDE)][:-1] + [(H - 1, 8, 3), (H - 1, 11, 3), (H - 1, 14, 2)]
@@ -28,7 +29,7 @@ LARGE_RING = 6
 SMALL_RING = 2
 PAIR = 2
 PAIRS = BLOCKS // PAIR
-PAIRS_AHEAD = 10
+PAIRS_AHEAD = 9
 BY_SCALAR = PAIRS - 1
 DIVIDE_BEHIND = 3
 FINISH_BEHIND = 4
@@ -74,8 +75,10 @@ def tile_multiheadgraphchannelattention_b_kernel(tc, table, w, a_src, a_dst, adj
         adj_pairs = adj_t.rearrange("(a k p) n -> a p k n", k=PAIR, p=P)
         for a in range(PAIRS):
             adj_rows = held.tile([P, PAIR, N], BF16, name=f"adj{a}")
-            nc.sync.dma_start(adj_rows[:], adj_pairs[a])
             adj.append(adj_rows)
+        for side in range(0, N, WIDE * P):
+            for a in range(PAIRS):
+                nc.sync.dma_start(adj[a][:, :, side : side + WIDE * P], adj_pairs[a][:, :, side : side + WIDE * P])
 
         ident_bf = held.tile([P, P], BF16, name="ident_bf")
         make_identity(nc, ident_bf[:])
@@ -86,7 +89,6 @@ def tile_multiheadgraphchannelattention_b_kernel(tc, table, w, a_src, a_dst, adj
         for q in range(H):
             blocks_t = held.tile([P, BLOCKS * ROW], BF16, name=f"hf_t{q}")
             nc.gpsimd.memset(runs_of(blocks_t, ROW)[:, :, O:ROW], 1.0)
-            nc.gpsimd.memset(runs_of(blocks_t, ROW)[:, :, O + 1 : O + 2], -1.0)
             hf_t.append(blocks_t)
 
         table_t = held.tile([D, S], BF16, name="table_t")
@@ -102,19 +104,6 @@ def tile_multiheadgraphchannelattention_b_kernel(tc, table, w, a_src, a_dst, adj
         def small_bank(shape, dtype, name):
             return psum.tile(shape, dtype, name=name, tag="small", bufs=SMALL_RING)
 
-        a_cols_ps = small_bank([P, 2 * H], BF16, "a_cols_ps")
-        nc.tensor.transpose(a_cols_ps[:], a_rows[0 : 2 * H, :], ident_bf[0 : 2 * H, 0 : 2 * H])
-        a_cols = held.tile([O, 2 * H], BF16, name="a_cols")
-        nc.vector.tensor_copy(a_cols[:], a_cols_ps[:])
-        a_src_wide = held.tile([O, H * P], BF16, name="a_src_wide")
-        turn = [held.tile([O, SUMS], BF16, name=f"turn{q}") for q in range(H)]
-        s_cols = [held.tile([P, 2 * BLOCKS], F32, name=f"s_cols{q}") for q in range(H)]
-        for q in range(H):
-            nc.vector.tensor_copy(a_src_wide[:, q * P : (q + 1) * P], a_cols[:, q : q + 1].to_broadcast([O, P]))
-            nc.vector.tensor_copy(turn[q][:, 0:P], ident_bf[:])
-            nc.vector.tensor_copy(turn[q][:, P : P + 1], a_cols[:, H + q : H + q + 1])
-            nc.vector.tensor_copy(turn[q][:, P + 1 : P + 2], a_cols[:, q : q + 1])
-
         for c in range(CHUNKS):
             flipped = large_bank([P, NODES_A_ROW * P], BF16, "flipped_chunk")
             for r in range(NODES_A_ROW):
@@ -125,6 +114,19 @@ def tile_multiheadgraphchannelattention_b_kernel(tc, table, w, a_src, a_dst, adj
                 nc.vector.tensor_copy(window_part, in_order)
             else:
                 nc.scalar.copy(window_part, in_order)
+
+        a_cols_ps = small_bank([P, 2 * H], BF16, "a_cols_ps")
+        nc.tensor.transpose(a_cols_ps[:], a_rows[0 : 2 * H, :], ident_bf[0 : 2 * H, 0 : 2 * H])
+        a_cols = held.tile([O, 2 * H], BF16, name="a_cols")
+        nc.vector.tensor_copy(a_cols[:], a_cols_ps[:])
+        a_src_wide = held.tile([O, H * P], BF16, name="a_src_wide")
+        turn = [held.tile([O, TURNED], BF16, name=f"turn{q}") for q in range(H)]
+        s_cols = [held.tile([P, 2 * BLOCKS], F32, name=f"s_cols{q}") for q in range(H)]
+        for q in range(H):
+            nc.vector.tensor_copy(a_src_wide[:, q * P : (q + 1) * P], a_cols[:, q : q + 1].to_broadcast([O, P]))
+            nc.vector.tensor_copy(turn[q][:, 0:P], ident_bf[:])
+            nc.vector.tensor_copy(turn[q][:, P : P + 1], a_cols[:, H + q : H + q + 1])
+            nc.vector.tensor_copy(turn[q][:, P + 1 : P + 2], a_cols[:, q : q + 1])
 
         def look_up(q, with_vector):
             for c in range(PIECES):
@@ -145,15 +147,18 @@ def tile_multiheadgraphchannelattention_b_kernel(tc, table, w, a_src, a_dst, adj
                 )
             nc.scalar.activation(c_row[q][:, c * PIECE : (c + 1) * PIECE], s_src[:], FUNC.Exp, scale=SLOPE - 1.0)
 
-        def turn_blocks(q, tb, bank):
+        def keep_turned(q, tb, blocks, by_block):
+            nc.scalar.copy(runs_of(hf_t[q], ROW)[:, tb : tb + blocks, 0:O], by_block[:, :, 0:O])
+
+        def turn_blocks(q, tb, bank, keep=True):
             blocks = min(A_BANK, BLOCKS - tb)
-            turned = bank([P, A_BANK * SUMS], F32, "turned")
+            turned = bank([P, A_BANK * TURNED], F32, "turned")
             for k in range(blocks):
                 nc.tensor.matmul(
-                    turned[:, k * SUMS : (k + 1) * SUMS], hf[q][:, (tb + k) * P : (tb + k + 1) * P], turn[q][:],
+                    turned[:, k * TURNED : (k + 1) * TURNED], hf[q][:, (tb + k) * P : (tb + k + 1) * P], turn[q][:],
                     start=True, stop=True,
                 )
-            by_block = runs_of(turned[:, 0 : blocks * SUMS], SUMS)
+            by_block = runs_of(turned[:, 0 : blocks * TURNED], TURNED)
             nc.scalar.activation(b_col[q][:, tb : tb + blocks].unsqueeze(2), by_block[:, :, P : P + 1], FUNC.Exp)
             nc.scalar.activation(
                 e_col[q][:, tb : tb + blocks].unsqueeze(2), by_block[:, :, P : P + 1], FUNC.Exp, scale=SLOPE
@@ -165,7 +170,9 @@ def tile_multiheadgraphchannelattention_b_kernel(tc, table, w, a_src, a_dst, adj
                         s_cols[q][:, side * BLOCKS + tb : side * BLOCKS + tb + blocks].unsqueeze(2),
                         by_block[:, :, column : column + 1],
                     )
-            nc.scalar.copy(runs_of(hf_t[q], ROW)[:, tb : tb + blocks, 0:O], by_block[:, :, 0:O])
+            if keep:
+                keep_turned(q, tb, blocks, by_block)
+            return q, tb, blocks, by_block
 
         s_rows = {}
 
@@ -208,15 +215,21 @@ def tile_multiheadgraphchannelattention_b_kernel(tc, table, w, a_src, a_dst, adj
                 if by_scalar and a == BY_SCALAR:
                     unmasked = from_scalar
                 else:
-                    unmasked = ring.tile([P, PAIR, WIDE * P], BF16, name="unmasked")
-                    for h in range(PAIR):
-                        tb = a * PAIR + h
-                        nc.vector.tensor_scalar(
-                            unmasked[:, h, 0:width], c_row[q][:, columns], e_col[q][:, tb : tb + 1],
-                            b_col[q][:, tb : tb + 1], ALU.mult, ALU.max,
-                        )
+                    unmasked = ring.tile([P, PAIR, WIDE * P], BF16, name="unmasked", bufs=3)
                 weights = ring.tile([P, PAIR, WIDE * P], BF16, name="weights", bufs=PAIRS_AHEAD)
-                nc.vector.tensor_tensor(weights[:, :, 0:width], unmasked[:, :, 0:width], adj[a][:, :, columns], ALU.mult)
+                cut = width // 2 if q == 0 and first == 0 and a == 0 else width
+                for c in range(0, width, cut):
+                    row_part = slice(first * P + c, first * P + c + cut)
+                    if not (by_scalar and a == BY_SCALAR):
+                        for h in range(PAIR):
+                            tb = a * PAIR + h
+                            nc.vector.tensor_scalar(
+                                unmasked[:, h, c : c + cut], c_row[q][:, row_part],
+                                e_col[q][:, tb : tb + 1], b_col[q][:, tb : tb + 1], ALU.mult, ALU.max,
+                            )
+                    nc.vector.tensor_tensor(
+                        weights[:, :, c : c + cut], unmasked[:, :, c : c + cut], adj[a][:, :, row_part], ALU.mult
+                    )
                 for h in range(PAIR):
                     tb = a * PAIR + h
                     for jb in range(blocks):
@@ -230,50 +243,32 @@ def tile_multiheadgraphchannelattention_b_kernel(tc, table, w, a_src, a_dst, adj
                         )
             return banks
 
-        def divide(sums, blocks, by_vector):
-            recip = ring.tile([P, A_BANK, 2], F32, name="recip", bufs=6)
-            nc.vector.reciprocal(recip[:, 0:blocks, :], runs_of(sums[:, 0 : blocks * SUMS], SUMS)[:, :, O : O + 2])
-            above = ring.tile([P, A_BANK * O], F32, name="above", bufs=6)
-            below = None if by_vector else ring.tile([P, A_BANK * O], F32, name="below", bufs=3)
-            for k in range(blocks):
-                numerators = sums[:, k * SUMS : k * SUMS + O]
-                if by_vector:
-                    nc.scalar.activation(above[:, k * O : (k + 1) * O], numerators, FUNC.Copy, scale=recip[:, k, 0:1])
-                else:
-                    nc.scalar.activation(above[:, k * O : (k + 1) * O], numerators, FUNC.Relu, scale=recip[:, k, 0:1])
-                    nc.scalar.activation(below[:, k * O : (k + 1) * O], numerators, FUNC.Relu, scale=recip[:, k, 1:2])
-            if not by_vector:
-                nc.scalar.activation(below[:, 0 : blocks * O], below[:, 0 : blocks * O], FUNC.Exp, scale=-1.0)
-            return [
-                (above[:, k * O : (k + 1) * O], None if by_vector else below[:, k * O : (k + 1) * O]) for k in range(blocks)
-            ]
-
-        def divide_unit(blocks, banks, by_vector, divided):
-            for b in range(len(banks)):
-                divided.extend(divide(banks[b], min(A_BANK, blocks - b * A_BANK), by_vector))
+        def divide_unit(blocks, banks, divided):
+            for b in range(0, blocks, A_BANK):
+                here = min(A_BANK, blocks - b)
+                sums = banks[b // A_BANK]
+                recip = ring.tile([P, A_BANK, 1], F32, name="recip", bufs=6)
+                nc.vector.reciprocal(recip[:, 0:here, :], runs_of(sums[:, 0 : here * SUMS], SUMS)[:, :, O : O + 1])
+                y = ring.tile([P, A_BANK * O], F32, name="y", bufs=6)
+                for k in range(here):
+                    nc.scalar.activation(
+                        y[:, k * O : (k + 1) * O], sums[:, k * SUMS : k * SUMS + O], FUNC.Copy, scale=recip[:, k, :]
+                    )
+                    divided.append(y[:, k * O : (k + 1) * O])
 
         def store(q, block, together, result):
             nc.sync.dma_start(
                 out[q * O : (q + 1) * O, block * P : (block + together) * P], result[:, 0 : together * P]
             )
 
-        def turn_results(q, first, done, together, by_vector, divided, halfway):
+        def turn_results(done, together, divided, halfway):
             y_t = small_bank([O, together * P], F32, "y_t")
             for k in range(together):
-                above, below = divided[done + k]
-                at = y_t[:, k * P : (k + 1) * P]
-                nc.tensor.matmul(at, above, ident_f[:], is_transpose=True, start=True, stop=by_vector)
-                if not by_vector:
-                    nc.tensor.matmul(at, below, ident_f[:], is_transpose=True, start=False, stop=True)
-            if by_vector:
-                e = ring.tile([O, PIECE], F32, name="e")
-                nc.scalar.activation(e[:, 0 : together * P], y_t[:], FUNC.Relu, scale=-1.0)
-                nc.scalar.activation(e[:, 0 : together * P], e[:, 0 : together * P], FUNC.Exp, scale=-1.0)
-                halfway[done] = (e, y_t)
-            else:
-                result = ring.tile([O, PIECE], F32, name="result", bufs=3)
-                nc.scalar.activation(result[:, 0 : together * P], y_t[:], FUNC.Copy, bias=-1.0)
-                store(q, first + done, together, result)
+                nc.tensor.transpose(y_t[:, k * P : (k + 1) * P], divided[done + k], ident_f[:])
+            e = ring.tile([O, PIECE], F32, name="e")
+            nc.scalar.activation(e[:, 0 : together * P], y_t[:], FUNC.Relu, scale=-1.0)
+            nc.scalar.activation(e[:, 0 : together * P], e[:, 0 : together * P], FUNC.Exp, scale=-1.0)
+            halfway[done] = (e, y_t)
 
         def end_elu(q, first, done, together, halfway):
             e, y_t = halfway[done]
@@ -285,11 +280,13 @@ def tile_multiheadgraphchannelattention_b_kernel(tc, table, w, a_src, a_dst, adj
 
         look_up(0, with_vector=True)
         of_first_unit = WIDE * P // PIECE
-        for c in range(of_first_unit):
-            score_rows(0, c, large_bank)
-        for tb in range(0, BLOCKS, A_BANK):
+        score_rows(0, 0, large_bank)
+        turned = turn_blocks(0, 0, large_bank, keep=False)
+        score_rows(0, 1, large_bank)
+        keep_turned(*turned)
+        for tb in range(A_BANK, BLOCKS, A_BANK):
             turn_blocks(0, tb, large_bank)
-        for c in range(of_first_unit, PIECES):
+        for c in range(2, PIECES):
             score_rows(0, c, large_bank)
         for q in range(H - 1, 0, -1):
             look_up(q, with_vector=False)
@@ -304,17 +301,13 @@ def tile_multiheadgraphchannelattention_b_kernel(tc, table, w, a_src, a_dst, adj
                 for h in range(2):
                     agenda[EXP_BEHIND + h].append(partial(exp_row, q + 1, h))
             banks = make_and_sum(q, first, blocks, u > 0, agenda)
-            by_vector = first == 0
             divided, halfway = [], {}
             agenda = {a: [] for a in range(PAIRS)}
-            agenda[DIVIDE_BEHIND].append(partial(divide_unit, blocks, banks, by_vector, divided))
+            agenda[DIVIDE_BEHIND].append(partial(divide_unit, blocks, banks, divided))
             for g, done in enumerate(range(0, blocks, A_RESULT)):
                 together = min(A_RESULT, blocks - done)
-                agenda[FINISH_BEHIND + g].append(
-                    partial(turn_results, q, first, done, together, by_vector, divided, halfway)
-                )
-                if by_vector:
-                    agenda[END_BEHIND + g].append(partial(end_elu, q, first, done, together, halfway))
+                agenda[FINISH_BEHIND + g].append(partial(turn_results, done, together, divided, halfway))
+                agenda[END_BEHIND + g].append(partial(end_elu, q, first, done, together, halfway))
         for a in range(PAIRS):
             for step in agenda[a]:
                 step()

@@ -23,18 +23,20 @@ TURNED = O + 2
 A_BANK = PIECE // TURNED
 HALF = PIECE // 2
 WIDE = 8
-UNITS = [(q, b, WIDE) for q in range(H) for b in (0, WIDE)][:-1] + [(H - 1, 8, 3), (H - 1, 11, 3), (H - 1, 14, 2)]
+UNITS = [(q, b, WIDE) for q in range(H) for b in (0, WIDE)][:-1] + [(H - 1, 8, 6), (H - 1, 14, 2)]
 A_RESULT = PIECE // P
 LARGE_RING = 6
 SMALL_RING = 2
+FOUR = 4
+FOURS = BLOCKS // FOUR
+FOURS_AHEAD = 4
 PAIR = 2
 PAIRS = BLOCKS // PAIR
-PAIRS_AHEAD = 9
-BY_SCALAR = PAIRS - 1
+BY_SCALAR = (13, 14, 15)
 DIVIDE_BEHIND = 3
 FINISH_BEHIND = 4
 END_BEHIND = 6
-TURN_BEHIND = 1
+SPREAD_BEHIND = 3
 EXP_BEHIND = 5
 
 FLOPS = 2 * D * H * O * N + 2 * 2 * H * O * N + 2 * H * N * N * (O + 1)
@@ -72,13 +74,13 @@ def tile_multiheadgraphchannelattention_b_kernel(tc, table, w, a_src, a_dst, adj
         nc.scalar.activation(warm[:], warm[:], FUNC.Exp)
 
         adj = []
-        adj_pairs = adj_t.rearrange("(a k p) n -> a p k n", k=PAIR, p=P)
-        for a in range(PAIRS):
-            adj_rows = held.tile([P, PAIR, N], BF16, name=f"adj{a}")
+        adj_fours = adj_t.rearrange("(f k p) n -> f p k n", k=FOUR, p=P)
+        for f in range(FOURS):
+            adj_rows = held.tile([P, FOUR, N], BF16, name=f"adj{f}")
             adj.append(adj_rows)
         for side in range(0, N, WIDE * P):
-            for a in range(PAIRS):
-                nc.sync.dma_start(adj[a][:, :, side : side + WIDE * P], adj_pairs[a][:, :, side : side + WIDE * P])
+            for f in range(FOURS):
+                nc.sync.dma_start(adj[f][:, :, side : side + WIDE * P], adj_fours[f][:, :, side : side + WIDE * P])
 
         ident_bf = held.tile([P, P], BF16, name="ident_bf")
         make_identity(nc, ident_bf[:])
@@ -150,6 +152,12 @@ def tile_multiheadgraphchannelattention_b_kernel(tc, table, w, a_src, a_dst, adj
         def keep_turned(q, tb, blocks, by_block):
             nc.scalar.copy(runs_of(hf_t[q], ROW)[:, tb : tb + blocks, 0:O], by_block[:, :, 0:O])
 
+        def exp_columns(q, tb, blocks, s_dst):
+            part = slice(tb, tb + blocks)
+            nc.scalar.activation(b_col[q][:, part].unsqueeze(2), s_dst, FUNC.Exp)
+            nc.scalar.activation(e_col[q][:, part].unsqueeze(2), s_dst, FUNC.Exp, scale=SLOPE)
+            nc.scalar.mul(minus_b_col[q][:, part], b_col[q][:, part], -1.0)
+
         def turn_blocks(q, tb, bank, keep=True):
             blocks = min(A_BANK, BLOCKS - tb)
             turned = bank([P, A_BANK * TURNED], F32, "turned")
@@ -159,17 +167,10 @@ def tile_multiheadgraphchannelattention_b_kernel(tc, table, w, a_src, a_dst, adj
                     start=True, stop=True,
                 )
             by_block = runs_of(turned[:, 0 : blocks * TURNED], TURNED)
-            nc.scalar.activation(b_col[q][:, tb : tb + blocks].unsqueeze(2), by_block[:, :, P : P + 1], FUNC.Exp)
-            nc.scalar.activation(
-                e_col[q][:, tb : tb + blocks].unsqueeze(2), by_block[:, :, P : P + 1], FUNC.Exp, scale=SLOPE
-            )
-            nc.scalar.mul(minus_b_col[q][:, tb : tb + blocks], b_col[q][:, tb : tb + blocks], -1.0)
-            if q > 0:
-                for side, column in ((0, P + 1), (1, P)):
-                    nc.scalar.copy(
-                        s_cols[q][:, side * BLOCKS + tb : side * BLOCKS + tb + blocks].unsqueeze(2),
-                        by_block[:, :, column : column + 1],
-                    )
+            if q == 0:
+                exp_columns(0, tb, blocks, by_block[:, :, P : P + 1])
+            else:
+                nc.scalar.copy(s_cols[q].rearrange("p (k b) -> p b k", k=2)[:, tb : tb + blocks, :], by_block[:, :, P:TURNED])
             if keep:
                 keep_turned(q, tb, blocks, by_block)
             return q, tb, blocks, by_block
@@ -177,12 +178,13 @@ def tile_multiheadgraphchannelattention_b_kernel(tc, table, w, a_src, a_dst, adj
         s_rows = {}
 
         def spread_row(q):
+            exp_columns(q, 0, BLOCKS, s_cols[q][:, 0:BLOCKS].unsqueeze(2))
             rows_ps = small_bank([2 * BLOCKS, P], F32, "rows_ps")
             nc.tensor.transpose(rows_ps[:], s_cols[q][:], ident_f[:])
             rows = ring.tile([2 * BLOCKS, P], F32, name="rows")
             nc.scalar.copy(rows[:], rows_ps[:])
             parked = (H - 1) * O + q
-            nc.sync.dma_start(out[parked, :].rearrange("(b p) -> b p", p=P), rows[0:BLOCKS, :])
+            nc.sync.dma_start(out[parked, :].rearrange("(b p) -> b p", p=P), rows[BLOCKS : 2 * BLOCKS, :])
             for h in range(2):
                 s_row = ring.tile([P, N // 2], F32, name="s_row")
                 nc.sync.dma_start(s_row[:], out[parked, h * N // 2 : (h + 1) * N // 2].partition_broadcast(P))
@@ -193,45 +195,45 @@ def tile_multiheadgraphchannelattention_b_kernel(tc, table, w, a_src, a_dst, adj
                 c_row[q][:, h * N // 2 : (h + 1) * N // 2], s_rows[q, h][:], FUNC.Exp, scale=SLOPE - 1.0
             )
 
-        def make_and_sum(q, first, blocks, by_scalar, agenda):
+        def make_and_sum(q, first, blocks, with_scalar, agenda):
             width = blocks * P
-            columns = slice(first * P, first * P + width)
             banks = [large_bank([P, A_BANK * SUMS], F32, "sums") for b in range(0, blocks, A_BANK)]
+            by_scalar = BY_SCALAR if with_scalar else ()
             if by_scalar:
-                from_scalar = ring.tile([P, PAIR, WIDE * P], BF16, name="from_scalar")
-                for h in range(PAIR):
-                    tb = BY_SCALAR * PAIR + h
-                    excess = ring.tile([P, WIDE * P], F32, name="excess")
-                    nc.scalar.activation(
-                        excess[:, 0:width], c_row[q][:, columns], FUNC.Relu,
-                        bias=minus_b_col[q][:, tb : tb + 1], scale=e_col[q][:, tb : tb + 1],
-                    )
-                    nc.scalar.activation(
-                        from_scalar[:, h, 0:width], excess[:, 0:width], FUNC.Identity, bias=b_col[q][:, tb : tb + 1]
-                    )
-            for a in range(PAIRS):
-                for step in agenda[a]:
-                    step()
-                if by_scalar and a == BY_SCALAR:
-                    unmasked = from_scalar
+                last_four = ring.tile([P, FOUR, WIDE * P], BF16, name="last_four")
+            for tb in by_scalar:
+                excess = ring.tile([P, WIDE * P], F32, name="excess")
+                nc.scalar.activation(
+                    excess[:, 0:width], c_row[q][:, first * P : first * P + width], FUNC.Relu,
+                    bias=minus_b_col[q][:, tb : tb + 1], scale=e_col[q][:, tb : tb + 1],
+                )
+                nc.scalar.activation(
+                    last_four[:, tb % FOUR, 0:width], excess[:, 0:width], FUNC.Identity, bias=b_col[q][:, tb : tb + 1]
+                )
+            for f in range(FOURS):
+                if by_scalar and f == FOURS - 1:
+                    unmasked = last_four
                 else:
-                    unmasked = ring.tile([P, PAIR, WIDE * P], BF16, name="unmasked", bufs=3)
-                weights = ring.tile([P, PAIR, WIDE * P], BF16, name="weights", bufs=PAIRS_AHEAD)
-                cut = width // 2 if q == 0 and first == 0 and a == 0 else width
+                    unmasked = ring.tile([P, FOUR, WIDE * P], BF16, name="unmasked")
+                weights = ring.tile([P, FOUR, WIDE * P], BF16, name="weights", bufs=FOURS_AHEAD)
+                cut = width // 2 if q == 0 and first == 0 and f == 0 else width
                 for c in range(0, width, cut):
-                    row_part = slice(first * P + c, first * P + c + cut)
-                    if not (by_scalar and a == BY_SCALAR):
-                        for h in range(PAIR):
-                            tb = a * PAIR + h
+                    part = slice(first * P + c, first * P + c + cut)
+                    for h in range(FOUR):
+                        tb = f * FOUR + h
+                        if c == 0 and tb % PAIR == 0:
+                            for step in agenda[tb // PAIR]:
+                                step()
+                        if tb not in by_scalar:
                             nc.vector.tensor_scalar(
-                                unmasked[:, h, c : c + cut], c_row[q][:, row_part],
+                                unmasked[:, h, c : c + cut], c_row[q][:, part],
                                 e_col[q][:, tb : tb + 1], b_col[q][:, tb : tb + 1], ALU.mult, ALU.max,
                             )
                     nc.vector.tensor_tensor(
-                        weights[:, :, c : c + cut], unmasked[:, :, c : c + cut], adj[a][:, :, row_part], ALU.mult
+                        weights[:, :, c : c + cut], unmasked[:, :, c : c + cut], adj[f][:, :, part], ALU.mult
                     )
-                for h in range(PAIR):
-                    tb = a * PAIR + h
+                for h in range(FOUR):
+                    tb = f * FOUR + h
                     for jb in range(blocks):
                         k = jb % A_BANK
                         nc.tensor.matmul(
@@ -261,13 +263,17 @@ def tile_multiheadgraphchannelattention_b_kernel(tc, table, w, a_src, a_dst, adj
                 out[q * O : (q + 1) * O, block * P : (block + together) * P], result[:, 0 : together * P]
             )
 
-        def turn_results(done, together, divided, halfway):
+        def turn_results(done, together, divided, halfway, vector_free):
             y_t = small_bank([O, together * P], F32, "y_t")
             for k in range(together):
                 nc.tensor.transpose(y_t[:, k * P : (k + 1) * P], divided[done + k], ident_f[:])
             e = ring.tile([O, PIECE], F32, name="e")
-            nc.scalar.activation(e[:, 0 : together * P], y_t[:], FUNC.Relu, scale=-1.0)
-            nc.scalar.activation(e[:, 0 : together * P], e[:, 0 : together * P], FUNC.Exp, scale=-1.0)
+            if vector_free:
+                nc.vector.tensor_scalar_min(e[:, 0 : together * P], y_t[:], 0.0)
+                nc.scalar.activation(e[:, 0 : together * P], e[:, 0 : together * P], FUNC.Exp)
+            else:
+                nc.scalar.activation(e[:, 0 : together * P], y_t[:], FUNC.Relu, scale=-1.0)
+                nc.scalar.activation(e[:, 0 : together * P], e[:, 0 : together * P], FUNC.Exp, scale=-1.0)
             halfway[done] = (e, y_t)
 
         def end_elu(q, first, done, together, halfway):
@@ -291,23 +297,27 @@ def tile_multiheadgraphchannelattention_b_kernel(tc, table, w, a_src, a_dst, adj
         for q in range(H - 1, 0, -1):
             look_up(q, with_vector=False)
 
-        agenda = {a: [] for a in range(PAIRS)}
+        agenda = {a: [] for a in range(PAIRS + 1)}
         for u, (q, first, blocks) in enumerate(UNITS):
             if q + 1 < H and first == 0:
                 for tb in range(0, BLOCKS, A_BANK):
-                    agenda[TURN_BEHIND + tb // A_BANK].append(partial(turn_blocks, q + 1, tb, small_bank))
-                agenda[PAIRS - 1].append(partial(spread_row, q + 1))
+                    agenda[tb // A_BANK // 2].append(partial(turn_blocks, q + 1, tb, small_bank))
+                agenda[SPREAD_BEHIND].append(partial(spread_row, q + 1))
             elif q + 1 < H:
                 for h in range(2):
                     agenda[EXP_BEHIND + h].append(partial(exp_row, q + 1, h))
             banks = make_and_sum(q, first, blocks, u > 0, agenda)
+            for step in agenda[PAIRS]:
+                step()
             divided, halfway = [], {}
-            agenda = {a: [] for a in range(PAIRS)}
-            agenda[DIVIDE_BEHIND].append(partial(divide_unit, blocks, banks, divided))
+            agenda = {a: [] for a in range(PAIRS + 1)}
+            ending = u + 2 >= len(UNITS)
+            divide_at, turn_at, end_at = (1, 2, PAIRS - 1) if ending else (DIVIDE_BEHIND, FINISH_BEHIND, END_BEHIND)
+            agenda[divide_at].append(partial(divide_unit, blocks, banks, divided))
             for g, done in enumerate(range(0, blocks, A_RESULT)):
                 together = min(A_RESULT, blocks - done)
-                agenda[FINISH_BEHIND + g].append(partial(turn_results, done, together, divided, halfway))
-                agenda[END_BEHIND + g].append(partial(end_elu, q, first, done, together, halfway))
-        for a in range(PAIRS):
+                agenda[turn_at + g].append(partial(turn_results, done, together, divided, halfway, ending))
+                agenda[end_at + g].append(partial(end_elu, q, first, done, together, halfway))
+        for a in range(PAIRS + 1):
             for step in agenda[a]:
                 step()

@@ -19,8 +19,7 @@ NODES_A_ROW = 4
 CHUNKS = S // (P * NODES_A_ROW)
 ROW = 144
 SUMS = O + 1
-TURNED = O + 2
-A_BANK = PIECE // TURNED
+A_BANK = PIECE // SUMS
 HALF = PIECE // 2
 WIDE = 8
 UNITS = [(q, b, WIDE) for q in range(H) for b in (0, WIDE)][:-1] + [(H - 1, 8, 6), (H - 1, 14, 2)]
@@ -32,12 +31,11 @@ FOURS = BLOCKS // FOUR
 FOURS_AHEAD = 4
 PAIR = 2
 PAIRS = BLOCKS // PAIR
-BY_SCALAR = (13, 14, 15)
+SCALAR_TILES = 2
 DIVIDE_BEHIND = 3
 FINISH_BEHIND = 4
-END_BEHIND = 6
-SPREAD_BEHIND = 3
-EXP_BEHIND = 5
+END_BEHIND = 7
+COLUMNS_BEHIND = 3
 
 FLOPS = 2 * D * H * O * N + 2 * 2 * H * O * N + 2 * H * N * N * (O + 1)
 
@@ -122,13 +120,12 @@ def tile_multiheadgraphchannelattention_b_kernel(tc, table, w, a_src, a_dst, adj
         a_cols = held.tile([O, 2 * H], BF16, name="a_cols")
         nc.vector.tensor_copy(a_cols[:], a_cols_ps[:])
         a_src_wide = held.tile([O, H * P], BF16, name="a_src_wide")
-        turn = [held.tile([O, TURNED], BF16, name=f"turn{q}") for q in range(H)]
-        s_cols = [held.tile([P, 2 * BLOCKS], F32, name=f"s_cols{q}") for q in range(H)]
+        turn = [held.tile([O, SUMS], BF16, name=f"turn{q}") for q in range(H)]
+        s_dst = [held.tile([P, BLOCKS], F32, name=f"s_dst{q}") for q in range(H)]
         for q in range(H):
             nc.vector.tensor_copy(a_src_wide[:, q * P : (q + 1) * P], a_cols[:, q : q + 1].to_broadcast([O, P]))
             nc.vector.tensor_copy(turn[q][:, 0:P], ident_bf[:])
             nc.vector.tensor_copy(turn[q][:, P : P + 1], a_cols[:, H + q : H + q + 1])
-            nc.vector.tensor_copy(turn[q][:, P + 1 : P + 2], a_cols[:, q : q + 1])
 
         def look_up(q, with_vector):
             for c in range(PIECES):
@@ -142,63 +139,44 @@ def tile_multiheadgraphchannelattention_b_kernel(tc, table, w, a_src, a_dst, adj
 
         def score_rows(q, c, bank):
             s_src = bank([P, PIECE], F32, "s_src")
-            for h in range(2):
+            step = HALF if q == 0 else PIECE
+            for h in range(0, PIECE, step):
                 nc.tensor.matmul(
-                    s_src[:, h * HALF : (h + 1) * HALF], a_src_wide[:, q * P : (q + 1) * P],
-                    hf[q][:, c * PIECE + h * HALF : c * PIECE + (h + 1) * HALF], start=True, stop=True,
+                    s_src[:, h : h + step], a_src_wide[:, q * P : (q + 1) * P],
+                    hf[q][:, c * PIECE + h : c * PIECE + h + step], start=True, stop=True,
                 )
             nc.scalar.activation(c_row[q][:, c * PIECE : (c + 1) * PIECE], s_src[:], FUNC.Exp, scale=SLOPE - 1.0)
 
         def keep_turned(q, tb, blocks, by_block):
             nc.scalar.copy(runs_of(hf_t[q], ROW)[:, tb : tb + blocks, 0:O], by_block[:, :, 0:O])
 
-        def exp_columns(q, tb, blocks, s_dst):
+        def exp_columns(q, tb, blocks, scores):
             part = slice(tb, tb + blocks)
-            nc.scalar.activation(b_col[q][:, part].unsqueeze(2), s_dst, FUNC.Exp)
-            nc.scalar.activation(e_col[q][:, part].unsqueeze(2), s_dst, FUNC.Exp, scale=SLOPE)
+            nc.scalar.activation(b_col[q][:, part].unsqueeze(2), scores, FUNC.Exp)
+            nc.scalar.activation(e_col[q][:, part].unsqueeze(2), scores, FUNC.Exp, scale=SLOPE)
             nc.scalar.mul(minus_b_col[q][:, part], b_col[q][:, part], -1.0)
 
         def turn_blocks(q, tb, bank, keep=True):
             blocks = min(A_BANK, BLOCKS - tb)
-            turned = bank([P, A_BANK * TURNED], F32, "turned")
+            turned = bank([P, A_BANK * SUMS], F32, "turned")
             for k in range(blocks):
                 nc.tensor.matmul(
-                    turned[:, k * TURNED : (k + 1) * TURNED], hf[q][:, (tb + k) * P : (tb + k + 1) * P], turn[q][:],
+                    turned[:, k * SUMS : (k + 1) * SUMS], hf[q][:, (tb + k) * P : (tb + k + 1) * P], turn[q][:],
                     start=True, stop=True,
                 )
-            by_block = runs_of(turned[:, 0 : blocks * TURNED], TURNED)
+            by_block = runs_of(turned[:, 0 : blocks * SUMS], SUMS)
             if q == 0:
                 exp_columns(0, tb, blocks, by_block[:, :, P : P + 1])
             else:
-                nc.scalar.copy(s_cols[q].rearrange("p (k b) -> p b k", k=2)[:, tb : tb + blocks, :], by_block[:, :, P:TURNED])
+                nc.scalar.copy(s_dst[q][:, tb : tb + blocks].unsqueeze(2), by_block[:, :, P : P + 1])
             if keep:
                 keep_turned(q, tb, blocks, by_block)
             return q, tb, blocks, by_block
 
-        s_rows = {}
-
-        def spread_row(q):
-            exp_columns(q, 0, BLOCKS, s_cols[q][:, 0:BLOCKS].unsqueeze(2))
-            rows_ps = small_bank([2 * BLOCKS, P], F32, "rows_ps")
-            nc.tensor.transpose(rows_ps[:], s_cols[q][:], ident_f[:])
-            rows = ring.tile([2 * BLOCKS, P], F32, name="rows")
-            nc.scalar.copy(rows[:], rows_ps[:])
-            parked = (H - 1) * O + q
-            nc.sync.dma_start(out[parked, :].rearrange("(b p) -> b p", p=P), rows[BLOCKS : 2 * BLOCKS, :])
-            for h in range(2):
-                s_row = ring.tile([P, N // 2], F32, name="s_row")
-                nc.sync.dma_start(s_row[:], out[parked, h * N // 2 : (h + 1) * N // 2].partition_broadcast(P))
-                s_rows[q, h] = s_row
-
-        def exp_row(q, h):
-            nc.scalar.activation(
-                c_row[q][:, h * N // 2 : (h + 1) * N // 2], s_rows[q, h][:], FUNC.Exp, scale=SLOPE - 1.0
-            )
-
-        def make_and_sum(q, first, blocks, with_scalar, agenda):
+        def make_and_sum(u, q, first, blocks, agenda):
             width = blocks * P
             banks = [large_bank([P, A_BANK * SUMS], F32, "sums") for b in range(0, blocks, A_BANK)]
-            by_scalar = BY_SCALAR if with_scalar else ()
+            by_scalar = range(BLOCKS - (SCALAR_TILES if u > 0 else 0), BLOCKS)
             if by_scalar:
                 last_four = ring.tile([P, FOUR, WIDE * P], BF16, name="last_four")
             for tb in by_scalar:
@@ -214,12 +192,13 @@ def tile_multiheadgraphchannelattention_b_kernel(tc, table, w, a_src, a_dst, adj
                 if by_scalar and f == FOURS - 1:
                     unmasked = last_four
                 else:
-                    unmasked = ring.tile([P, FOUR, WIDE * P], BF16, name="unmasked")
+                    unmasked = ring.tile([P, FOUR, WIDE * P], BF16, name="unmasked", bufs=3)
                 weights = ring.tile([P, FOUR, WIDE * P], BF16, name="weights", bufs=FOURS_AHEAD)
                 cut = width // 2 if q == 0 and first == 0 and f == 0 else width
-                for c in range(0, width, cut):
+                tiles = PAIR if u + 1 == len(UNITS) else FOUR
+                for h0, c in [(h0, c) for h0 in range(0, FOUR, tiles) for c in range(0, width, cut)]:
                     part = slice(first * P + c, first * P + c + cut)
-                    for h in range(FOUR):
+                    for h in range(h0, h0 + tiles):
                         tb = f * FOUR + h
                         if c == 0 and tb % PAIR == 0:
                             for step in agenda[tb // PAIR]:
@@ -230,7 +209,8 @@ def tile_multiheadgraphchannelattention_b_kernel(tc, table, w, a_src, a_dst, adj
                                 e_col[q][:, tb : tb + 1], b_col[q][:, tb : tb + 1], ALU.mult, ALU.max,
                             )
                     nc.vector.tensor_tensor(
-                        weights[:, :, c : c + cut], unmasked[:, :, c : c + cut], adj[f][:, :, part], ALU.mult
+                        weights[:, h0 : h0 + tiles, c : c + cut], unmasked[:, h0 : h0 + tiles, c : c + cut],
+                        adj[f][:, h0 : h0 + tiles, part], ALU.mult,
                     )
                 for h in range(FOUR):
                     tb = f * FOUR + h
@@ -302,11 +282,11 @@ def tile_multiheadgraphchannelattention_b_kernel(tc, table, w, a_src, a_dst, adj
             if q + 1 < H and first == 0:
                 for tb in range(0, BLOCKS, A_BANK):
                     agenda[tb // A_BANK // 2].append(partial(turn_blocks, q + 1, tb, small_bank))
-                agenda[SPREAD_BEHIND].append(partial(spread_row, q + 1))
+                agenda[COLUMNS_BEHIND].append(partial(exp_columns, q + 1, 0, BLOCKS, s_dst[q + 1][:].unsqueeze(2)))
             elif q + 1 < H:
-                for h in range(2):
-                    agenda[EXP_BEHIND + h].append(partial(exp_row, q + 1, h))
-            banks = make_and_sum(q, first, blocks, u > 0, agenda)
+                for c in range(PIECES):
+                    agenda[c].append(partial(score_rows, q + 1, c, small_bank))
+            banks = make_and_sum(u, q, first, blocks, agenda)
             for step in agenda[PAIRS]:
                 step()
             divided, halfway = [], {}

@@ -31,7 +31,6 @@ FOURS = BLOCKS // FOUR
 FOURS_AHEAD = 4
 PAIR = 2
 PAIRS = BLOCKS // PAIR
-SCALAR_TILES = 2
 DIVIDE_BEHIND = 3
 FINISH_BEHIND = 4
 END_BEHIND = 7
@@ -176,7 +175,7 @@ def tile_multiheadgraphchannelattention_b_kernel(tc, table, w, a_src, a_dst, adj
         def make_and_sum(u, q, first, blocks, agenda):
             width = blocks * P
             banks = [large_bank([P, A_BANK * SUMS], F32, "sums") for b in range(0, blocks, A_BANK)]
-            by_scalar = range(BLOCKS - (SCALAR_TILES if u > 0 else 0), BLOCKS)
+            by_scalar = range(BLOCKS - (0 if u == 0 else 2 if first == 0 else 3), BLOCKS)
             if by_scalar:
                 last_four = ring.tile([P, FOUR, WIDE * P], BF16, name="last_four")
             for tb in by_scalar:

from functools import partial

import concourse.mybir as mybir
from concourse.masks import make_identity

BF16 = mybir.dt.bfloat16
F32 = mybir.dt.float32
U16 = mybir.dt.uint16
FUNC = mybir.ActivationFunctionType
ALU = mybir.AluOpType

P = 128
S, D, H, O, N = 4096, 128, 4, 128, 2048
SLOPE = 0.2
PIECE = 512
PIECES = N // PIECE
BLOCKS = N // P
NODES_A_ROW = 4
CHUNKS = S // (P * NODES_A_ROW)
ROW = 144
SUMS = O + 1
A_BANK = PIECE // SUMS
HALF = PIECE // 2
WIDE = 8
UNITS = [(q, b, WIDE) for q in range(H) for b in (0, WIDE)][:-1] + [(H - 1, 8, 6), (H - 1, 14, 2)]
A_RESULT = PIECE // P
LARGE_RING = 6
SMALL_RING = 2
FOUR = 4
FOURS = BLOCKS // FOUR
FOURS_AHEAD = 4
PAIR = 2
PAIRS = BLOCKS // PAIR
DIVIDE_BEHIND = 3
FINISH_BEHIND = 4
END_BEHIND = 7
COLUMNS_BEHIND = 3

FLOPS = 2 * D * H * O * N + 2 * 2 * H * O * N + 2 * H * N * N * (O + 1)


def runs_of(ap, width):
    return ap.rearrange("p (r k) -> p r k", k=width)


def tile_multiheadgraphchannelattention_b_kernel(tc, table, w, a_src, a_dst, adj_t, offs, out):
    nc = tc.nc
    with (
        tc.tile_pool(name="lists", bufs=1) as lists,
        tc.tile_pool(name="held", bufs=1) as held,
        tc.tile_pool(name="ring", bufs=2) as ring,
        tc.psum_pool(name="psum", bufs=SMALL_RING) as psum,
    ):
        offsets = lists.tile([P, N // 16], U16, name="offsets")
        nc.sync.dma_start(offsets[:], offs)

        table_chunks = table.rearrange("(c p r) d -> c p r d", p=P, r=NODES_A_ROW)
        raw_chunks = []
        for c in range(CHUNKS):
            raw = ring.tile([P, NODES_A_ROW, D], BF16, name="raw", bufs=CHUNKS)
            nc.sync.dma_start(raw[:], table_chunks[c])
            raw_chunks.append(raw)

        proj = held.tile([D, H * O], BF16, name="proj")
        nc.scalar.dma_start(proj[:], w)
        a_rows = held.tile([P, O], BF16, name="a_rows")
        nc.scalar.dma_start(a_rows[0:H, :], a_src.rearrange("(q o) one -> q (o one)", q=H))
        nc.scalar.dma_start(a_rows[H : 2 * H, :], a_dst.rearrange("(q o) one -> q (o one)", q=H))
        warm = held.tile([P, 1], F32, name="warm")
        nc.vector.memset(warm[:], 0.0)
        nc.scalar.activation(warm[:], warm[:], FUNC.Exp)

        adj = []
        adj_fours = adj_t.rearrange("(f k p) n -> f p k n", k=FOUR, p=P)
        for f in range(FOURS):
            adj_rows = held.tile([P, FOUR, N], BF16, name=f"adj{f}")
            adj.append(adj_rows)
        for side in range(0, N, WIDE * P):
            for f in range(FOURS):
                nc.sync.dma_start(adj[f][:, :, side : side + WIDE * P], adj_fours[f][:, :, side : side + WIDE * P])

        ident_bf = held.tile([P, P], BF16, name="ident_bf")
        make_identity(nc, ident_bf[:])
        ident_f = held.tile([P, P], F32, name="ident_f")
        make_identity(nc, ident_f[:])

        hf_t = []
        for q in range(H):
            blocks_t = held.tile([P, BLOCKS * ROW], BF16, name=f"hf_t{q}")
            nc.gpsimd.memset(runs_of(blocks_t, ROW)[:, :, O:ROW], 1.0)
            hf_t.append(blocks_t)

        table_t = held.tile([D, S], BF16, name="table_t")
        hf = [held.tile([O, N], BF16, name=f"hf{q}") for q in range(H)]
        c_row = [held.tile([P, N], BF16, name=f"c_row{q}") for q in range(H)]
        b_col = [held.tile([P, BLOCKS], F32, name=f"b_col{q}") for q in range(H)]
        e_col = [held.tile([P, BLOCKS], F32, name=f"e_col{q}") for q in range(H)]
        minus_b_col = [held.tile([P, BLOCKS], F32, name=f"minus_b_col{q}") for q in range(H)]

        def large_bank(shape, dtype, name):
            return psum.tile(shape, dtype, name=name, tag="large", bufs=LARGE_RING)

        def small_bank(shape, dtype, name):
            return psum.tile(shape, dtype, name=name, tag="small", bufs=SMALL_RING)

        for c in range(CHUNKS):
            flipped = large_bank([P, NODES_A_ROW * P], BF16, "flipped_chunk")
            for r in range(NODES_A_ROW):
                nc.tensor.transpose(flipped[:, r * P : (r + 1) * P], raw_chunks[c][:, r, :], ident_bf[:])
            in_order = flipped.rearrange("d (r p) -> d p r", p=P)
            window_part = runs_of(table_t[:, c * NODES_A_ROW * P : (c + 1) * NODES_A_ROW * P], NODES_A_ROW)
            if c % 2 == 0:
                nc.vector.tensor_copy(window_part, in_order)
            else:
                nc.scalar.copy(window_part, in_order)

        a_cols_ps = small_bank([P, 2 * H], BF16, "a_cols_ps")
        nc.tensor.transpose(a_cols_ps[:], a_rows[0 : 2 * H, :], ident_bf[0 : 2 * H, 0 : 2 * H])
        a_cols = held.tile([O, 2 * H], BF16, name="a_cols")
        nc.vector.tensor_copy(a_cols[:], a_cols_ps[:])
        a_src_wide = held.tile([O, H * P], BF16, name="a_src_wide")
        turn = [held.tile([O, SUMS], BF16, name=f"turn{q}") for q in range(H)]
        s_dst = [held.tile([P, BLOCKS], F32, name=f"s_dst{q}") for q in range(H)]
        for q in range(H):
            nc.vector.tensor_copy(a_src_wide[:, q * P : (q + 1) * P], a_cols[:, q : q + 1].to_broadcast([O, P]))
            nc.vector.tensor_copy(turn[q][:, 0:P], ident_bf[:])
            nc.vector.tensor_copy(turn[q][:, P : P + 1], a_cols[:, H + q : H + q + 1])

        def look_up(q, with_vector):
            for c in range(PIECES):
                picked = table_t[:].indirect(offsets[:, c * (PIECE // 16) : (c + 1) * (PIECE // 16)])
                product = large_bank([O, PIECE], F32, "product")
                nc.tensor.matmul(product[:], proj[:, q * O : (q + 1) * O], picked, start=True, stop=True)
                if with_vector:
                    nc.vector.tensor_copy(hf[q][:, c * PIECE : (c + 1) * PIECE], product[:])
                else:
                    nc.scalar.copy(hf[q][:, c * PIECE : (c + 1) * PIECE], product[:])

        def score_rows(q, c, bank):
            s_src = bank([P, PIECE], F32, "s_src")
            step = HALF if q == 0 else PIECE
            for h in range(0, PIECE, step):
                nc.tensor.matmul(
                    s_src[:, h : h + step], a_src_wide[:, q * P : (q + 1) * P],
                    hf[q][:, c * PIECE + h : c * PIECE + h + step], start=True, stop=True,
                )
            nc.scalar.activation(c_row[q][:, c * PIECE : (c + 1) * PIECE], s_src[:], FUNC.Exp, scale=SLOPE - 1.0)

        def keep_turned(q, tb, blocks, by_block):
            nc.scalar.copy(runs_of(hf_t[q], ROW)[:, tb : tb + blocks, 0:O], by_block[:, :, 0:O])

        def exp_columns(q, tb, blocks, scores):
            part = slice(tb, tb + blocks)
            nc.scalar.activation(b_col[q][:, part].unsqueeze(2), scores, FUNC.Exp)
            nc.scalar.activation(e_col[q][:, part].unsqueeze(2), scores, FUNC.Exp, scale=SLOPE)
            nc.scalar.mul(minus_b_col[q][:, part], b_col[q][:, part], -1.0)

        def turn_blocks(q, tb, bank, keep=True):
            blocks = min(A_BANK, BLOCKS - tb)
            turned = bank([P, A_BANK * SUMS], F32, "turned")
            for k in range(blocks):
                nc.tensor.matmul(
                    turned[:, k * SUMS : (k + 1) * SUMS], hf[q][:, (tb + k) * P : (tb + k + 1) * P], turn[q][:],
                    start=True, stop=True,
                )
            by_block = runs_of(turned[:, 0 : blocks * SUMS], SUMS)
            if q == 0:
                exp_columns(0, tb, blocks, by_block[:, :, P : P + 1])
            else:
                nc.scalar.copy(s_dst[q][:, tb : tb + blocks].unsqueeze(2), by_block[:, :, P : P + 1])
            if keep:
                keep_turned(q, tb, blocks, by_block)
            return q, tb, blocks, by_block

        def make_and_sum(u, q, first, blocks, agenda):
            width = blocks * P
            banks = [large_bank([P, A_BANK * SUMS], F32, "sums") for b in range(0, blocks, A_BANK)]
            by_scalar = range(BLOCKS - (0 if u == 0 else 2 if first == 0 else 3), BLOCKS)
            if by_scalar:
                last_four = ring.tile([P, FOUR, WIDE * P], BF16, name="last_four")
            for tb in by_scalar:
                excess = ring.tile([P, WIDE * P], F32, name="excess")
                nc.scalar.activation(
                    excess[:, 0:width], c_row[q][:, first * P : first * P + width], FUNC.Relu,
                    bias=minus_b_col[q][:, tb : tb + 1], scale=e_col[q][:, tb : tb + 1],
                )
                nc.scalar.activation(
                    last_four[:, tb % FOUR, 0:width], excess[:, 0:width], FUNC.Identity, bias=b_col[q][:, tb : tb + 1]
                )
            for f in range(FOURS):
                if by_scalar and f == FOURS - 1:
                    unmasked = last_four
                else:
                    unmasked = ring.tile([P, FOUR, WIDE * P], BF16, name="unmasked", bufs=3)
                weights = ring.tile([P, FOUR, WIDE * P], BF16, name="weights", bufs=FOURS_AHEAD)
                cut = width // 2 if q == 0 and first == 0 and f == 0 else width
                tiles = PAIR if u + 1 == len(UNITS) else FOUR
                for h0, c in [(h0, c) for h0 in range(0, FOUR, tiles) for c in range(0, width, cut)]:
                    part = slice(first * P + c, first * P + c + cut)
                    for h in range(h0, h0 + tiles):
                        tb = f * FOUR + h
                        if c == 0 and tb % PAIR == 0:
                            for step in agenda[tb // PAIR]:
                                step()
                        if tb not in by_scalar:
                            nc.vector.tensor_scalar(
                                unmasked[:, h, c : c + cut], c_row[q][:, part],
                                e_col[q][:, tb : tb + 1], b_col[q][:, tb : tb + 1], ALU.mult, ALU.max,
                            )
                    nc.vector.tensor_tensor(
                        weights[:, h0 : h0 + tiles, c : c + cut], unmasked[:, h0 : h0 + tiles, c : c + cut],
                        adj[f][:, h0 : h0 + tiles, part], ALU.mult,
                    )
                for h in range(FOUR):
                    tb = f * FOUR + h
                    for jb in range(blocks):
                        k = jb % A_BANK
                        nc.tensor.matmul(
                            banks[jb // A_BANK][:, k * SUMS : (k + 1) * SUMS],
                            weights[:, h, jb * P : (jb + 1) * P],
                            hf_t[q][:, tb * ROW : tb * ROW + SUMS],
                            start=(tb == 0 and k == 0),
                            stop=(tb == BLOCKS - 1 and (k == A_BANK - 1 or jb == blocks - 1)),
                        )
            return banks

        def divide_unit(blocks, banks, divided):
            for b in range(0, blocks, A_BANK):
                here = min(A_BANK, blocks - b)
                sums = banks[b // A_BANK]
                recip = ring.tile([P, A_BANK, 1], F32, name="recip", bufs=6)
                nc.vector.reciprocal(recip[:, 0:here, :], runs_of(sums[:, 0 : here * SUMS], SUMS)[:, :, O : O + 1])
                y = ring.tile([P, A_BANK * O], F32, name="y", bufs=6)
                for k in range(here):
                    nc.scalar.activation(
                        y[:, k * O : (k + 1) * O], sums[:, k * SUMS : k * SUMS + O], FUNC.Copy, scale=recip[:, k, :]
                    )
                    divided.append(y[:, k * O : (k + 1) * O])

        def store(q, block, together, result):
            nc.sync.dma_start(
                out[q * O : (q + 1) * O, block * P : (block + together) * P], result[:, 0 : together * P]
            )

        def turn_results(done, together, divided, halfway, vector_free):
            y_t = small_bank([O, together * P], F32, "y_t")
            for k in range(together):
                nc.tensor.transpose(y_t[:, k * P : (k + 1) * P], divided[done + k], ident_f[:])
            e = ring.tile([O, PIECE], F32, name="e")
            if vector_free:
                nc.vector.tensor_scalar_min(e[:, 0 : together * P], y_t[:], 0.0)
                nc.scalar.activation(e[:, 0 : together * P], e[:, 0 : together * P], FUNC.Exp)
            else:
                nc.scalar.activation(e[:, 0 : together * P], y_t[:], FUNC.Relu, scale=-1.0)
                nc.scalar.activation(e[:, 0 : together * P], e[:, 0 : together * P], FUNC.Exp, scale=-1.0)
            halfway[done] = (e, y_t)

        def end_elu(q, first, done, together, halfway):
            e, y_t = halfway[done]
            result = ring.tile([O, PIECE], F32, name="result", bufs=3)
            nc.vector.scalar_tensor_tensor(
                result[:, 0 : together * P], e[:, 0 : together * P], -1.0, y_t[:], ALU.add, ALU.max
            )
            store(q, first + done, together, result)

        look_up(0, with_vector=True)
        of_first_unit = WIDE * P // PIECE
        score_rows(0, 0, large_bank)
        turned = turn_blocks(0, 0, large_bank, keep=False)
        score_rows(0, 1, large_bank)
        keep_turned(*turned)
        for tb in range(A_BANK, BLOCKS, A_BANK):
            turn_blocks(0, tb, large_bank)
        for c in range(2, PIECES):
            score_rows(0, c, large_bank)
        for q in range(H - 1, 0, -1):
            look_up(q, with_vector=False)

        agenda = {a: [] for a in range(PAIRS + 1)}
        for u, (q, first, blocks) in enumerate(UNITS):
            if q + 1 < H and first == 0:
                for tb in range(0, BLOCKS, A_BANK):
                    agenda[tb // A_BANK // 2].append(partial(turn_blocks, q + 1, tb, small_bank))
                agenda[COLUMNS_BEHIND].append(partial(exp_columns, q + 1, 0, BLOCKS, s_dst[q + 1][:].unsqueeze(2)))
            elif q + 1 < H:
                for c in range(PIECES):
                    agenda[c].append(partial(score_rows, q + 1, c, small_bank))
            banks = make_and_sum(u, q, first, blocks, agenda)
            for step in agenda[PAIRS]:
                step()
            divided, halfway = [], {}
            agenda = {a: [] for a in range(PAIRS + 1)}
            ending = u + 2 >= len(UNITS)
            divide_at, turn_at, end_at = (1, 2, PAIRS - 1) if ending else (DIVIDE_BEHIND, FINISH_BEHIND, END_BEHIND)
            agenda[divide_at].append(partial(divide_unit, blocks, banks, divided))
            for g, done in enumerate(range(0, blocks, A_RESULT)):
                together = min(A_RESULT, blocks - done)
                agenda[turn_at + g].append(partial(turn_results, done, together, divided, halfway, ending))
                agenda[end_at + g].append(partial(end_elu, q, first, done, together, halfway))
        for a in range(PAIRS + 1):
            for step in agenda[a]:
                step()
